import numpy as np
import ml_dtypes


def mxq(x, axis, fmt="e4m3"):
    dtype, down = {"e4m3": (ml_dtypes.float8_e4m3fn, 7), "e5m2": (ml_dtypes.float8_e5m2, 14)}[fmt]
    v = np.moveaxis(np.asarray(x, np.float32).astype(ml_dtypes.bfloat16).astype(np.float64), axis, -1)
    blocks = v.reshape(v.shape[:-1] + (-1, 32))
    amax = np.abs(blocks).max(-1, keepdims=True)
    byte = np.maximum(np.where(amax > 0, np.frexp(amax)[1] - 1 + 127, 0) - down, 1)
    scale = np.exp2(byte - 127.0)
    codes = (blocks / scale).astype(np.float32).astype(dtype).astype(np.float64)
    return np.moveaxis((codes * scale).reshape(v.shape), -1, axis)


WIDE = False


def mx_kscale(k):
    if not WIDE:
        return np.ones(k)
    levels = np.array([10, -10, 5, -5, 0])
    if k % 512:
        return np.exp2(np.random.permutation(np.resize(levels, k // 32))).repeat(32)
    a = np.empty((k // 512, 16))
    for p in range(k // 512):
        a[p, :8] = np.random.permutation(np.resize(levels, 8))
        for g in range(8):
            far = levels[np.abs(levels - a[p, g]) >= 10]
            a[p, g + 8] = far[np.random.randint(len(far))]
    return np.exp2(a.ravel()).repeat(32)


BF16 = ml_dtypes.bfloat16


def bf(x):
    return np.asarray(x, np.float32).astype(BF16)


def f64(x):
    return np.asarray(x).astype(np.float64)


B, N, C, F = 4, 32, 1024, 1024
EPS_STD = 1e-5


def draw0():
    u, s = mx_kscale(C), mx_kscale(C)
    rows = np.concatenate([u, u, s])
    return {"x": bf(np.random.standard_normal((B, N, C)) * u),
            "e_enc": bf(np.random.standard_normal((B, N, N, C)) * s),
            "W_pre": bf(np.random.standard_normal((3 * C, F)) / np.sqrt(3 * C) / rows[:, None]),
            "b_pre": bf(np.random.standard_normal(F) * 0.3)}


def core(x, e_enc, W_pre, b_pre):
    w = f64(W_pre)
    xq = mxq(f64(x), 2, "e4m3")
    tgt = xq @ mxq(w[:C], 0, "e4m3")
    src = xq @ mxq(w[C:2 * C], 0, "e4m3")
    edg = mxq(f64(e_enc), 3, "e4m3") @ mxq(w[2 * C:], 0, "e4m3")
    m = tgt[:, :, None, :] + src[:, None, :, :] + edg + f64(b_pre)
    mean = m.mean(axis=2)
    mn = m.min(axis=2)
    mx = m.max(axis=2)
    var = (m * m).mean(axis=2) - mean * mean
    std = np.sqrt(np.maximum(var, 0.0) + EPS_STD)
    return np.concatenate([mean, mn, mx, std], axis=-1)


def e4m3fn_bytes(y):
    return np.clip(np.asarray(y, np.float64), -448.0, 448.0).astype(np.float32).astype(ml_dtypes.float8_e4m3fn).view(np.uint8)


def e4m3fn_values(b):
    return np.asarray(b, np.uint8).view(ml_dtypes.float8_e4m3fn).astype(np.float64)


def setup_inputs():
    d = draw0()
    x0 = np.asarray(d['e_enc']).astype(np.float64)
    s = (np.max(np.abs(x0), axis=(0, 1, 2), keepdims=True) / 448.0).astype(np.float32)
    out = {}
    for k, v in d.items():
        if k == 'e_enc':
            out['e_enc_bytes'] = e4m3fn_bytes(x0 / s.astype(np.float64))
            out['e_enc_scale'] = s
        else:
            out[k] = v
    return out


def reference(x, e_enc_bytes, e_enc_scale, W_pre, b_pre):
    return core(x, e4m3fn_values(e_enc_bytes) * e_enc_scale.astype(np.float64), W_pre, b_pre)

@@ -1,0 +1,349 @@
+from contextlib import ExitStack
+
+import concourse.mybir as mybir
+from concourse.masks import make_identity
+
+B, N, C, F = 4, 32, 1024, 1024
+EPS_STD = 1e-5
+FLOPS = 2 * (B * N * N + 2 * B * N) * C * F
+
+F32 = mybir.dt.float32
+BF16 = mybir.dt.bfloat16
+U32 = mybir.dt.uint32
+I32 = mybir.dt.int32
+U8 = mybir.dt.uint8
+FP8 = mybir.dt.float8_e4m3fn
+X4 = mybir.dt.float8_e4m3fn_x4
+ALU = mybir.AluOpType
+ACT = mybir.ActivationFunctionType
+AX = mybir.AxisListType
+
+P = 128
+CV = 336
+W_URGENT = ((4, 0), (5, 0), (2, 0), (3, 0), (4, 1), (5, 1), (2, 1), (3, 1))
+W_LATE = ((0, 0), (1, 0), (0, 1), (1, 1))
+
+
+def tile_gnnlayer_pa_kernel(tc, x, e_enc_bytes, e_enc_scale, W_pre, b_pre, out):
+    nc = tc.nc
+    e_view = e_enc_bytes.rearrange("b i j k -> (b i j) k").rearrange("(n t p) k -> n p t k", t=4, p=P)
+    w_view = W_pre.rearrange("(s p t) f -> s p t f", p=P, t=4)
+
+    with ExitStack() as ctx:
+        const = ctx.enter_context(tc.tile_pool(name="const", bufs=1))
+        wstage = ctx.enter_context(tc.tile_pool(name="wstage", bufs=4))
+        wgpool = ctx.enter_context(tc.tile_pool(name="wgpool", bufs=2))
+        ebpool = ctx.enter_context(tc.tile_pool(name="ebpool", bufs=3))
+        ebfpool = ctx.enter_context(tc.tile_pool(name="ebfpool", bufs=2))
+        egpool = ctx.enter_context(tc.tile_pool(name="egpool", bufs=1))
+        treepool = ctx.enter_context(tc.tile_pool(name="treepool", bufs=1))
+        ecpool = ctx.enter_context(tc.tile_pool(name="ecpool", bufs=2))
+        xrpool = ctx.enter_context(tc.tile_pool(name="xrpool", bufs=2))
+        sqpool = ctx.enter_context(tc.tile_pool(name="sqpool", bufs=2))
+        gpool = ctx.enter_context(tc.tile_pool(name="gpool", bufs=2))
+        ps_tp = ctx.enter_context(tc.psum_pool(name="ps_tp", bufs=2))
+        ps_acc = ctx.enter_context(tc.psum_pool(name="ps_acc", bufs=4))
+        ps_sum = ctx.enter_context(tc.psum_pool(name="ps_sum", bufs=1))
+        ps_fin = ctx.enter_context(tc.psum_pool(name="ps_fin", bufs=1))
+
+        ident = const.tile([P, P], F32, name="ident")
+        make_identity(nc, ident[:])
+        warm = const.tile([P, 2], F32, name="warm")
+        nc.vector.memset(warm[:], 1.0)
+        nc.scalar.activation(out=warm[:, 1:2], in_=warm[:, 0:1], func=ACT.Sqrt)
+
+        scl = const.tile([P, C], F32, name="scl")
+        nc.scalar.dma_start(out=scl[:], in_=e_enc_scale.rearrange("a b c k -> (a b c k)").partition_broadcast(P))
+        x_sb = const.tile([P, C], BF16, name="x_sb")
+        nc.sync.dma_start(out=x_sb[:], in_=x.rearrange("b n c -> (b n) c"))
+        bias_bf = const.tile([P, 8], BF16, name="bias_bf")
+        with nc.allow_non_contiguous_dma(reason="1024 bias values, one to a partition for each f tile"):
+            nc.scalar.dma_start(out=bias_bf[:], in_=b_pre.rearrange("(t p) -> p t", p=P))
+        bias_f = const.tile([P, 8], F32, name="bias_f")
+
+        eb = {}
+        wraw = {}
+
+        def load_e(rb):
+            eb[rb] = ebpool.tile([P, 4, C], U8, name="ebytes%d" % rb, tag="ebytes")
+            nc.sync.dma_start(out=eb[rb][:], in_=e_view[rb])
+
+        def load_w(s, fh):
+            wraw[(s, fh)] = wstage.tile([P, 4, 512], BF16, name="wraw%d_%d" % (s, fh), tag="wraw")
+            nc.sync.dma_start(out=wraw[(s, fh)][:], in_=w_view[s][:, :, 512 * fh : 512 * (fh + 1)])
+
+        load_e(0)
+        for s, fh in W_URGENT[0:4]:
+            load_w(s, fh)
+        load_e(1)
+        for s, fh in W_URGENT[4:8]:
+            load_w(s, fh)
+        load_e(2)
+
+        wc = {}
+        ws = {}
+        for s in range(6):
+            wc[s] = const.tile([P, F], U32, name="wc%d" % s, align_bytes=64)
+            ws[s] = const.tile([P, F], U8, name="ws%d" % s, align_bytes=64)
+
+        def prep_w(s, fh, cv):
+            raw = wraw[(s, fh)]
+            wg = wgpool.tile([P, 512, 4], BF16, name="wg%d_%d" % (s, fh), tag="wg", align_bytes=64)
+            if cv > 0:
+                nc.vector.tensor_copy(out=wg[:, 0:cv, :], in_=raw[:, :, 0:cv].rearrange("p t f -> p f t"))
+            nc.scalar.copy(out=wg[:, cv:512, :], in_=raw[:, :, cv:512].rearrange("p t f -> p f t"))
+            cols = slice(512 * fh, 512 * (fh + 1))
+            nc.vector.quantize_mx(
+                out=wc[s][:, cols].bitcast(X4), scales=ws[s][:, cols], in_=wg[:].rearrange("p f t -> p (f t)")
+            )
+
+        xw = x_sb[:].bitcast(F32)
+        xt = ps_tp.tile([P, 4, P], F32, name="xt", tag="tp")
+        for g in range(2):
+            for u in range(2):
+                nc.tensor.transpose(xt[:, 2 * g + u, :], xw[:, 256 * g + u : 256 * (g + 1) : 2], ident[:])
+        xg = const.tile([P, 2 * P * 4], BF16, name="xg", align_bytes=64)
+        xg_w = xg[:].bitcast(F32).rearrange("p (g r u) -> p g r u", g=2, u=2)
+        nc.scalar.copy(out=xg_w, in_=xt[:].rearrange("p (g u) r -> p g r u", u=2))
+        xc = const.tile([P, 2 * P], U32, name="xc", align_bytes=64)
+        xs = const.tile([P, 2 * P], U8, name="xs", align_bytes=64)
+        nc.vector.memset(xs[:].bitcast(I32), 0)
+        nc.vector.quantize_mx(out=xc[:].bitcast(X4), scales=xs[:], in_=xg[:])
+
+        xrc = {}
+        xrs = {}
+
+        def rep_x(b):
+            xrc[b] = xrpool.tile([P, 1024], U32, name="xrc%d" % b, tag="xrc", align_bytes=64)
+            xrs[b] = xrpool.tile([P, 1024], U8, name="xrs%d" % b, tag="xrs", align_bytes=64)
+            for g in range(2):
+                one = slice(g * P + b * N, g * P + (b + 1) * N)
+                nc.vector.tensor_copy(
+                    out=xrc[b][:, g * 512 : (g + 1) * 512].bitcast(I32).rearrange("p (c j) -> p c j", c=16),
+                    in_=xc[:, one].bitcast(I32).unsqueeze(1).to_broadcast([P, 16, N]),
+                )
+                nc.vector.tensor_copy(
+                    out=xrs[b][:, g * 512 : (g + 1) * 512].bitcast(I32).rearrange("p (c j) -> p c j", c=16),
+                    in_=xs[:, one].bitcast(I32).unsqueeze(1).to_broadcast([P, 16, N // 4]),
+                )
+
+        ebf = {}
+        eg = {}
+        ec = {}
+        es = {}
+
+        def widen(rb):
+            ebf[rb] = ebfpool.tile([P, 4, C], BF16, name="ebf%d" % rb, tag="ebf")
+            for tl in range(4):
+                nc.vector.tensor_tensor(
+                    out=ebf[rb][:, tl, :], in0=eb[rb][:, tl, :].bitcast(FP8), in1=scl[:], op=ALU.mult
+                )
+
+        def turn(rb, g):
+            if g == 0:
+                eg[rb] = egpool.tile([P, 2 * 512 * 4], BF16, name="eg%d" % rb, tag="eg", align_bytes=64)
+            eg_w = eg[rb][:].bitcast(F32).rearrange("p (g t r u) -> p g t r u", g=2, t=4, u=2)
+            for pair in range(2):
+                tp = ps_tp.tile([P, 2, 2, P], F32, name="tp", tag="tp")
+                for ti in range(2):
+                    words = ebf[rb][:, 2 * pair + ti, :].bitcast(F32)
+                    for u in range(2):
+                        nc.tensor.transpose(tp[:, ti, u, :], words[:, 256 * g + u : 256 * (g + 1) : 2], ident[:])
+                nc.scalar.copy(
+                    out=eg_w[:, g, 2 * pair : 2 * pair + 2], in_=tp[:].rearrange("p t u r -> p t r u")
+                )
+
+        def quant_e(rb):
+            ec[rb] = ecpool.tile([P, 1024], U32, name="ec%d" % rb, tag="ec", align_bytes=64)
+            es[rb] = ecpool.tile([P, 1024], U8, name="es%d" % rb, tag="es", align_bytes=64)
+            nc.vector.quantize_mx(out=ec[rb][:].bitcast(X4), scales=es[rb][:], in_=eg[rb][:])
+
+        tb = const.tile([P, 8, P], F32, name="tb")
+
+        def target_term():
+            nc.vector.tensor_copy(out=bias_f[:], in_=bias_bf[:])
+            for q2 in range(2):
+                tg = ps_fin.tile([P, 4, P], F32, name="tg", tag="fin")
+                for q in range(4):
+                    cols = slice((4 * q2 + q) * P, (4 * q2 + q + 1) * P)
+                    for g in range(2):
+                        nc.tensor.matmul_mx(
+                            out=tg[:, q, :],
+                            lhsT=wc[g][:, cols].bitcast(X4),
+                            lhsT_scale=ws[g][:, cols],
+                            rhs=xc[:, g * P : (g + 1) * P].bitcast(X4),
+                            rhs_scale=xs[:, g * P : (g + 1) * P],
+                            start=(g == 0),
+                            stop=(g == 1),
+                        )
+                for q in range(4):
+                    ft = 4 * q2 + q
+                    nc.scalar.activation(
+                        out=tb[:, ft, :], in_=tg[:, q, :], func=ACT.Identity, bias=bias_f[:, ft : ft + 1]
+                    )
+
+        res = {}
+        var = {}
+        msq = {}
+        sq = {}
+        sp = {}
+
+        def bank(rb, ft):
+            b, h = rb // 2, rb % 2
+            cols = slice(ft * P, (ft + 1) * P)
+            acc = ps_acc.tile([P, 512], F32, name="acc", tag="acc")
+            for g in range(2):
+                nc.tensor.matmul_mx(
+                    out=acc[:],
+                    lhsT=wc[4 + g][:, cols].bitcast(X4),
+                    lhsT_scale=ws[4 + g][:, cols],
+                    rhs=ec[rb][:, g * 512 : (g + 1) * 512].bitcast(X4),
+                    rhs_scale=es[rb][:, g * 512 : (g + 1) * 512],
+                    start=(g == 0),
+                    stop=False,
+                )
+            for g in range(2):
+                nc.tensor.matmul_mx(
+                    out=acc[:],
+                    lhsT=wc[2 + g][:, cols].bitcast(X4),
+                    lhsT_scale=ws[2 + g][:, cols],
+                    rhs=xrc[b][:, g * 512 : (g + 1) * 512].bitcast(X4),
+                    rhs_scale=xrs[b][:, g * 512 : (g + 1) * 512],
+                    start=False,
+                    stop=(g == 1),
+                )
+            by_j = acc[:].rearrange("p (c j) -> p j c", j=N)
+            nc.scalar.copy(out=sq[rb][:, 1, :, 16 * ft : 16 * (ft + 1)], in_=by_j)
+            nc.scalar.activation(out=sq[rb][:, 0, :, 16 * ft : 16 * (ft + 1)], in_=by_j, func=ACT.Square)
+
+        def trees(rb, f0, f1):
+            b, h = rb // 2, rb % 2
+            c0 = 16 * h
+            cs = slice(16 * f0, 16 * f1)
+            z = sq[rb]
+            tmax = treepool.tile([P, 16, P], F32, name="tmax", tag="tmax")
+            tmin = treepool.tile([P, 16, P], F32, name="tmin", tag="tmin")
+            both = ((tmax, ALU.max, 2), (tmin, ALU.min, 1))
+            for t, op, a in both:
+                nc.vector.tensor_tensor(out=t[:, 0:16, cs], in0=z[:, 1, 0:16, cs], in1=z[:, 1, 16:32, cs], op=op)
+            for n in (8, 4, 2):
+                for t, op, a in both:
+                    nc.vector.tensor_tensor(out=t[:, 0:n, cs], in0=t[:, 0:n, cs], in1=t[:, n : 2 * n, cs], op=op)
+            for t, op, a in both:
+                nc.vector.tensor_tensor(
+                    out=res[b][:, f0:f1, a, c0 : c0 + 16],
+                    in0=t[:, 0, cs].rearrange("p (f c) -> p f c", c=16),
+                    in1=t[:, 1, cs].rearrange("p (f c) -> p f c", c=16),
+                    op=op,
+                )
+
+        def fold_squares(rb):
+            nc.vector.tensor_tensor(
+                out=sq[rb][:, 0, 0:16, :], in0=sq[rb][:, 0, 0:16, :], in1=sq[rb][:, 0, 16:32, :], op=ALU.add
+            )
+
+        sum_order = [(1, j, N) for j in range(N)] + [(0, j, N // 2) for j in range(N // 2)]
+
+        def sum_run(rb, part):
+            if part == 0:
+                sp[rb] = ps_sum.tile([P, 2, P], F32, name="sp", tag="sp")
+            for q, j, n in sum_order[12 * part : 12 * (part + 1)]:
+                nc.tensor.matmul(
+                    out=sp[rb][:, q, :], lhsT=sq[rb][:, q, j, :], rhs=ident[:], is_transpose=True,
+                    start=(j == 0), stop=(j == n - 1),
+                )
+
+        def sums_back(rb):
+            b, h = rb // 2, rb % 2
+            c0 = 16 * h
+            s2 = gpool.tile([P, 2, P], F32, name="s2", tag="s2")
+            nc.scalar.copy(out=s2[:], in_=sp[rb][:])
+            bk = ps_fin.tile([P, 2, P], F32, name="bk", tag="fin")
+            for q in range(2):
+                nc.tensor.transpose(bk[:, q, :], s2[:, q, :], ident[:])
+            s_z = bk[:, 1, :].rearrange("p (f c) -> p f c", c=16)
+            s_zz = bk[:, 0, :].rearrange("p (f c) -> p f c", c=16)
+            nc.scalar.activation(out=res[b][:, :, 0, c0 : c0 + 16], in_=s_z, func=ACT.Copy, scale=1.0 / N)
+            nc.scalar.activation(out=msq[b][:, :, c0 : c0 + 16], in_=s_z, func=ACT.Square, scale=1.0 / N)
+            nc.vector.scalar_tensor_tensor(
+                out=var[b][:, :, c0 : c0 + 16], in0=s_zz, scalar=1.0 / N, in1=msq[b][:, :, c0 : c0 + 16],
+                op0=ALU.mult, op1=ALU.subtract,
+            )
+
+        def finish(b):
+            r = res[b]
+            nc.vector.tensor_scalar(
+                out=var[b][:], in0=var[b][:], scalar1=0.0, scalar2=EPS_STD, op0=ALU.max, op1=ALU.add
+            )
+            nc.scalar.activation(out=r[:, :, 3, :], in_=var[b][:], func=ACT.Sqrt)
+            nc.vector.tensor_tensor(
+                out=r[:, :, 0:3, :], in0=r[:, :, 0:3, :],
+                in1=tb[:, :, b * N : (b + 1) * N].unsqueeze(2).to_broadcast([P, 8, 3, N]), op=ALU.add,
+            )
+            o_sb = gpool.tile([P, F], F32, name="o_sb", tag="o_sb")
+            for q2 in range(2):
+                fin = ps_fin.tile([P, 4, P], F32, name="fin", tag="fin")
+                for q in range(4):
+                    nc.tensor.transpose(fin[:, q, :], r[:, 4 * q2 + q, :, :].rearrange("p a c -> p (a c)"), ident[:])
+                nc.scalar.copy(out=o_sb[:, 512 * q2 : 512 * (q2 + 1)], in_=fin[:].rearrange("p q f -> p (q f)"))
+            for a in range(4):
+                nc.sync.dma_start(out=out[b, :, a * F : (a + 1) * F], in_=o_sb[a * N : (a + 1) * N, :])
+
+        widen(0)
+        rep_x(0)
+        turn(0, 0)
+        turn(0, 1)
+        for s, fh in W_URGENT[0:2]:
+            prep_w(s, fh, CV)
+        quant_e(0)
+        for s, fh in W_URGENT[2:4]:
+            prep_w(s, fh, CV)
+        for s, fh in W_URGENT[4:8]:
+            prep_w(s, fh, 0)
+        widen(1)
+        for rb in range(8):
+            b = rb // 2
+            if rb % 2 == 0:
+                res[b] = gpool.tile([P, 8, 4, N], F32, name="res%d" % b, tag="res")
+                var[b] = gpool.tile([P, 8, N], F32, name="var%d" % b, tag="var")
+                msq[b] = gpool.tile([P, 8, N], F32, name="msq%d" % b, tag="msq")
+            sq[rb] = sqpool.tile([P, 2, N, P], F32, name="sq%d" % rb, tag="sq")
+            if rb + 3 < 8:
+                load_e(rb + 3)
+            if rb == 0:
+                for s, fh in W_LATE:
+                    load_w(s, fh)
+            if rb + 2 < 8:
+                widen(rb + 2)
+            if rb >= 1:
+                fold_squares(rb - 1)
+                trees(rb - 1, 0, 8)
+            for half in range(2):
+                if rb + 1 < 8:
+                    turn(rb + 1, half)
+                for pair in range(2):
+                    if rb >= 1:
+                        sum_run(rb - 1, 2 * half + pair)
+                    bank(rb, 4 * half + 2 * pair)
+                    bank(rb, 4 * half + 2 * pair + 1)
+                if rb == 7:
+                    if half == 1:
+                        fold_squares(rb)
+                    trees(rb, 4 * half, 4 * half + 4)
+            if rb + 1 < 8:
+                quant_e(rb + 1)
+            if rb >= 1:
+                sums_back(rb - 1)
+                if rb % 2 == 0:
+                    finish(b - 1)
+            if rb < 2:
+                for s, fh in W_LATE[2 * rb : 2 * rb + 2]:
+                    prep_w(s, fh, 0)
+            if rb == 1:
+                target_term()
+            if rb % 2 == 0 and b + 1 < B:
+                rep_x(b + 1)
+        for part in range(4):
+            sum_run(7, part)
+        sums_back(7)
+        finish(3)

@@ -1,7 +1,7 @@
 from contextlib import ExitStack
 
 import concourse.mybir as mybir
-from concourse.masks import make_identity
+from concourse.masks import make_block_diagonal, make_identity
 
 B, N, C, F = 4, 32, 1024, 1024
 EPS_STD = 1e-5
@@ -16,18 +16,22 @@ FP8 = mybir.dt.float8_e4m3fn
 X4 = mybir.dt.float8_e4m3fn_x4
 ALU = mybir.AluOpType
 ACT = mybir.ActivationFunctionType
-AX = mybir.AxisListType
 
 P = 128
+H = 512
+JT = 4
+NSTEP = N // JT
 CV = 336
+CG = 128
 W_URGENT = ((4, 0), (5, 0), (2, 0), (3, 0), (4, 1), (5, 1), (2, 1), (3, 1))
 W_LATE = ((0, 0), (1, 0), (0, 1), (1, 1))
 
 
 def tile_gnnlayer_pa_kernel(tc, x, e_enc_bytes, e_enc_scale, W_pre, b_pre, out):
     nc = tc.nc
-    e_view = e_enc_bytes.rearrange("b i j k -> (b i j) k").rearrange("(n t p) k -> n p t k", t=4, p=P)
+    e_view = e_enc_bytes.rearrange("b i (n t) k -> n (b i) t k", t=JT)
     w_view = W_pre.rearrange("(s p t) f -> s p t f", p=P, t=4)
+    out_view = out.rearrange("b i (a f) -> (b i) a f", a=4)
 
     with ExitStack() as ctx:
         const = ctx.enter_context(tc.tile_pool(name="const", bufs=1))
@@ -35,42 +39,37 @@ def tile_gnnlayer_pa_kernel(tc, x, e_enc_bytes, e_enc_scale, W_pre, b_pre, out):
         wgpool = ctx.enter_context(tc.tile_pool(name="wgpool", bufs=2))
         ebpool = ctx.enter_context(tc.tile_pool(name="ebpool", bufs=3))
         ebfpool = ctx.enter_context(tc.tile_pool(name="ebfpool", bufs=2))
-        egpool = ctx.enter_context(tc.tile_pool(name="egpool", bufs=1))
-        treepool = ctx.enter_context(tc.tile_pool(name="treepool", bufs=1))
+        egpool = ctx.enter_context(tc.tile_pool(name="egpool", bufs=2))
         ecpool = ctx.enter_context(tc.tile_pool(name="ecpool", bufs=2))
         xrpool = ctx.enter_context(tc.tile_pool(name="xrpool", bufs=2))
-        sqpool = ctx.enter_context(tc.tile_pool(name="sqpool", bufs=2))
-        gpool = ctx.enter_context(tc.tile_pool(name="gpool", bufs=2))
+        sqpool = ctx.enter_context(tc.tile_pool(name="sqpool", bufs=4))
         ps_tp = ctx.enter_context(tc.psum_pool(name="ps_tp", bufs=2))
         ps_acc = ctx.enter_context(tc.psum_pool(name="ps_acc", bufs=4))
         ps_sum = ctx.enter_context(tc.psum_pool(name="ps_sum", bufs=1))
-        ps_fin = ctx.enter_context(tc.psum_pool(name="ps_fin", bufs=1))
 
         ident = const.tile([P, P], F32, name="ident")
         make_identity(nc, ident[:])
+        blk = const.tile([P, P], F32, name="blk")
+        make_block_diagonal(nc, blk[:], N)
+        scl = const.tile([P, C], F32, name="scl")
+        nc.scalar.dma_start(out=scl[:], in_=e_enc_scale.rearrange("a b c k -> (a b c k)").partition_broadcast(P))
         warm = const.tile([P, 2], F32, name="warm")
         nc.vector.memset(warm[:], 1.0)
         nc.scalar.activation(out=warm[:, 1:2], in_=warm[:, 0:1], func=ACT.Sqrt)
-
-        scl = const.tile([P, C], F32, name="scl")
-        nc.scalar.dma_start(out=scl[:], in_=e_enc_scale.rearrange("a b c k -> (a b c k)").partition_broadcast(P))
         x_sb = const.tile([P, C], BF16, name="x_sb")
         nc.sync.dma_start(out=x_sb[:], in_=x.rearrange("b n c -> (b n) c"))
-        bias_bf = const.tile([P, 8], BF16, name="bias_bf")
-        with nc.allow_non_contiguous_dma(reason="1024 bias values, one to a partition for each f tile"):
-            nc.scalar.dma_start(out=bias_bf[:], in_=b_pre.rearrange("(t p) -> p t", p=P))
-        bias_f = const.tile([P, 8], F32, name="bias_f")
+        bias_bc = const.tile([P, F], BF16, name="bias_bc")
 
         eb = {}
         wraw = {}
 
-        def load_e(rb):
-            eb[rb] = ebpool.tile([P, 4, C], U8, name="ebytes%d" % rb, tag="ebytes")
-            nc.sync.dma_start(out=eb[rb][:], in_=e_view[rb])
+        def load_e(st):
+            eb[st] = ebpool.tile([P, JT, C], U8, name="ebytes%d" % st, tag="ebytes")
+            nc.sync.dma_start(out=eb[st][:], in_=e_view[st])
 
         def load_w(s, fh):
-            wraw[(s, fh)] = wstage.tile([P, 4, 512], BF16, name="wraw%d_%d" % (s, fh), tag="wraw")
-            nc.sync.dma_start(out=wraw[(s, fh)][:], in_=w_view[s][:, :, 512 * fh : 512 * (fh + 1)])
+            wraw[(s, fh)] = wstage.tile([P, 4, H], BF16, name="wraw%d_%d" % (s, fh), tag="wraw")
+            nc.sync.dma_start(out=wraw[(s, fh)][:], in_=w_view[s][:, :, H * fh : H * (fh + 1)])
 
         load_e(0)
         for s, fh in W_URGENT[0:4]:
@@ -86,13 +85,17 @@ def tile_gnnlayer_pa_kernel(tc, x, e_enc_bytes, e_enc_scale, W_pre, b_pre, out):
             wc[s] = const.tile([P, F], U32, name="wc%d" % s, align_bytes=64)
             ws[s] = const.tile([P, F], U8, name="ws%d" % s, align_bytes=64)
 
-        def prep_w(s, fh, cv):
+        def prep_w(s, fh, cv, cg):
             raw = wraw[(s, fh)]
-            wg = wgpool.tile([P, 512, 4], BF16, name="wg%d_%d" % (s, fh), tag="wg", align_bytes=64)
+            wg = wgpool.tile([P, H, 4], BF16, name="wg%d_%d" % (s, fh), tag="wg", align_bytes=64)
             if cv > 0:
                 nc.vector.tensor_copy(out=wg[:, 0:cv, :], in_=raw[:, :, 0:cv].rearrange("p t f -> p f t"))
-            nc.scalar.copy(out=wg[:, cv:512, :], in_=raw[:, :, cv:512].rearrange("p t f -> p f t"))
-            cols = slice(512 * fh, 512 * (fh + 1))
+            if cg > 0:
+                nc.gpsimd.tensor_copy(
+                    out=wg[:, cv : cv + cg, :], in_=raw[:, :, cv : cv + cg].rearrange("p t f -> p f t")
+                )
+            nc.scalar.copy(out=wg[:, cv + cg : H, :], in_=raw[:, :, cv + cg : H].rearrange("p t f -> p f t"))
+            cols = slice(H * fh, H * (fh + 1))
             nc.vector.quantize_mx(
                 out=wc[s][:, cols].bitcast(X4), scales=ws[s][:, cols], in_=wg[:].rearrange("p f t -> p (f t)")
             )
@@ -109,22 +112,27 @@ def tile_gnnlayer_pa_kernel(tc, x, e_enc_bytes, e_enc_scale, W_pre, b_pre, out):
         xs = const.tile([P, 2 * P], U8, name="xs", align_bytes=64)
         nc.vector.memset(xs[:].bitcast(I32), 0)
         nc.vector.quantize_mx(out=xc[:].bitcast(X4), scales=xs[:], in_=xg[:])
+        xs4 = const.tile([P, 4 * 2 * P], U8, name="xs4", align_bytes=64)
+        for r in range(4):
+            nc.vector.tensor_copy(out=xs4[:].rearrange("p (c r) -> p c r", r=4)[:, :, r], in_=xs[:])
 
         xrc = {}
         xrs = {}
 
-        def rep_x(b):
-            xrc[b] = xrpool.tile([P, 1024], U32, name="xrc%d" % b, tag="xrc", align_bytes=64)
-            xrs[b] = xrpool.tile([P, 1024], U8, name="xrs%d" % b, tag="xrs", align_bytes=64)
+        def rep_x(st):
+            xrc[st] = xrpool.tile([P, JT * 2 * P], U32, name="xrc%d" % st, tag="xrc", align_bytes=64)
+            xrs[st] = xrpool.tile([P, JT * 2 * P], U8, name="xrs%d" % st, tag="xrs", align_bytes=64)
+            js = slice(JT * st, JT * (st + 1))
             for g in range(2):
-                one = slice(g * P + b * N, g * P + (b + 1) * N)
-                nc.vector.tensor_copy(
-                    out=xrc[b][:, g * 512 : (g + 1) * 512].bitcast(I32).rearrange("p (c j) -> p c j", c=16),
-                    in_=xc[:, one].bitcast(I32).unsqueeze(1).to_broadcast([P, 16, N]),
+                one = slice(g * P, (g + 1) * P)
+                nc.gpsimd.tensor_copy(
+                    out=xrc[st][:].rearrange("p (t g b i) -> p t g b i", t=JT, g=2, b=B)[:, :, g],
+                    in_=xc[:, one].rearrange("p (b j) -> p j b", b=B)[:, js, :].unsqueeze(3).to_broadcast([P, JT, B, N]),
                 )
-                nc.vector.tensor_copy(
-                    out=xrs[b][:, g * 512 : (g + 1) * 512].bitcast(I32).rearrange("p (c j) -> p c j", c=16),
-                    in_=xs[:, one].bitcast(I32).unsqueeze(1).to_broadcast([P, 16, N // 4]),
+                nc.gpsimd.tensor_copy(
+                    out=xrs[st][:].bitcast(U32).rearrange("p (t g b w) -> p t g b w", t=JT, g=2, b=B)[:, :, g],
+                    in_=xs4[:].bitcast(U32)[:, one].rearrange("p (b j) -> p j b", b=B)[:, js, :]
+                    .unsqueeze(3).to_broadcast([P, JT, B, N // 4]),
                 )
 
         ebf = {}
@@ -132,218 +140,213 @@ def tile_gnnlayer_pa_kernel(tc, x, e_enc_bytes, e_enc_scale, W_pre, b_pre, out):
         ec = {}
         es = {}
 
-        def widen(rb):
-            ebf[rb] = ebfpool.tile([P, 4, C], BF16, name="ebf%d" % rb, tag="ebf")
-            for tl in range(4):
-                nc.vector.tensor_tensor(
-                    out=ebf[rb][:, tl, :], in0=eb[rb][:, tl, :].bitcast(FP8), in1=scl[:], op=ALU.mult
-                )
+        def widen(st, tl):
+            if tl == 0:
+                ebf[st] = ebfpool.tile([P, JT, C], BF16, name="ebf%d" % st, tag="ebf")
+            nc.vector.tensor_tensor(
+                out=ebf[st][:, tl, :], in0=eb[st][:, tl, :].bitcast(FP8), in1=scl[:], op=ALU.mult
+            )
 
-        def turn(rb, g):
-            if g == 0:
-                eg[rb] = egpool.tile([P, 2 * 512 * 4], BF16, name="eg%d" % rb, tag="eg", align_bytes=64)
-            eg_w = eg[rb][:].bitcast(F32).rearrange("p (g t r u) -> p g t r u", g=2, t=4, u=2)
-            for pair in range(2):
-                tp = ps_tp.tile([P, 2, 2, P], F32, name="tp", tag="tp")
-                for ti in range(2):
-                    words = ebf[rb][:, 2 * pair + ti, :].bitcast(F32)
-                    for u in range(2):
-                        nc.tensor.transpose(tp[:, ti, u, :], words[:, 256 * g + u : 256 * (g + 1) : 2], ident[:])
-                nc.scalar.copy(
-                    out=eg_w[:, g, 2 * pair : 2 * pair + 2], in_=tp[:].rearrange("p t u r -> p t r u")
-                )
+        def turn(st, tl):
+            if tl == 0:
+                eg[st] = egpool.tile([P, JT * 2 * P * 4], BF16, name="eg%d" % st, tag="eg", align_bytes=64)
+            eg_w = eg[st][:].bitcast(F32).rearrange("p (t g r u) -> p t g r u", t=JT, g=2, u=2)
+            words = ebf[st][:, tl, :].bitcast(F32)
+            tp = ps_tp.tile([P, 2, 2, P], F32, name="tp", tag="tp")
+            for g in range(2):
+                for u in range(2):
+                    nc.tensor.transpose(tp[:, g, u, :], words[:, 256 * g + u : 256 * (g + 1) : 2], ident[:])
+            nc.scalar.copy(out=eg_w[:, tl], in_=tp[:].rearrange("p g u r -> p g r u"))
 
-        def quant_e(rb):
-            ec[rb] = ecpool.tile([P, 1024], U32, name="ec%d" % rb, tag="ec", align_bytes=64)
-            es[rb] = ecpool.tile([P, 1024], U8, name="es%d" % rb, tag="es", align_bytes=64)
-            nc.vector.quantize_mx(out=ec[rb][:].bitcast(X4), scales=es[rb][:], in_=eg[rb][:])
+        def quant_e(st, t0, t1):
+            if t0 == 0:
+                ec[st] = ecpool.tile([P, JT * 2 * P], U32, name="ec%d" % st, tag="ec", align_bytes=64)
+                es[st] = ecpool.tile([P, JT * 2 * P], U8, name="es%d" % st, tag="es", align_bytes=64)
+            cols = slice(t0 * 2 * P, t1 * 2 * P)
+            nc.vector.quantize_mx(
+                out=ec[st][:, cols].bitcast(X4), scales=es[st][:, cols], in_=eg[st][:, t0 * 8 * P : t1 * 8 * P]
+            )
 
-        tb = const.tile([P, 8, P], F32, name="tb")
+        tb = const.tile([P, F], F32, name="tb")
+        src_sb = const.tile([P, F], F32, name="src_sb")
+        smean = const.tile([P, F], F32, name="smean")
 
-        def target_term():
-            nc.vector.tensor_copy(out=bias_f[:], in_=bias_bf[:])
-            for q2 in range(2):
-                tg = ps_fin.tile([P, 4, P], F32, name="tg", tag="fin")
-                for q in range(4):
-                    cols = slice((4 * q2 + q) * P, (4 * q2 + q + 1) * P)
-                    for g in range(2):
-                        nc.tensor.matmul_mx(
-                            out=tg[:, q, :],
-                            lhsT=wc[g][:, cols].bitcast(X4),
-                            lhsT_scale=ws[g][:, cols],
-                            rhs=xc[:, g * P : (g + 1) * P].bitcast(X4),
-                            rhs_scale=xs[:, g * P : (g + 1) * P],
-                            start=(g == 0),
-                            stop=(g == 1),
-                        )
-                for q in range(4):
-                    ft = 4 * q2 + q
-                    nc.scalar.activation(
-                        out=tb[:, ft, :], in_=tg[:, q, :], func=ACT.Identity, bias=bias_f[:, ft : ft + 1]
-                    )
-
-        res = {}
-        var = {}
-        msq = {}
-        sq = {}
-        sp = {}
-
-        def bank(rb, ft):
-            b, h = rb // 2, rb % 2
-            cols = slice(ft * P, (ft + 1) * P)
-            acc = ps_acc.tile([P, 512], F32, name="acc", tag="acc")
+        def x_product(s0, fh):
+            cols = slice(H * fh, H * (fh + 1))
+            pr = ps_acc.tile([P, H], F32, name="pr", tag="acc")
             for g in range(2):
                 nc.tensor.matmul_mx(
-                    out=acc[:],
-                    lhsT=wc[4 + g][:, cols].bitcast(X4),
-                    lhsT_scale=ws[4 + g][:, cols],
-                    rhs=ec[rb][:, g * 512 : (g + 1) * 512].bitcast(X4),
-                    rhs_scale=es[rb][:, g * 512 : (g + 1) * 512],
+                    out=pr[:],
+                    lhsT=xc[:, g * P : (g + 1) * P].bitcast(X4),
+                    lhsT_scale=xs[:, g * P : (g + 1) * P],
+                    rhs=wc[s0 + g][:, cols].bitcast(X4),
+                    rhs_scale=ws[s0 + g][:, cols],
                     start=(g == 0),
-                    stop=False,
+                    stop=(g == 1),
                 )
+            return pr
+
+        def target_term(fh):
+            cols = slice(H * fh, H * (fh + 1))
+            pr = x_product(0, fh)
+            nc.vector.tensor_tensor(out=tb[:, cols], in0=pr[:], in1=bias_bc[:, cols], op=ALU.add)
+
+        def source_mean(fh):
+            cols = slice(H * fh, H * (fh + 1))
+            pr = x_product(2, fh)
+            nc.scalar.copy(out=src_sb[:, cols], in_=pr[:])
+            sm = ps_acc.tile([P, H], F32, name="sm", tag="acc")
+            nc.tensor.matmul(out=sm[:], lhsT=blk[:], rhs=src_sb[:, cols], start=True, stop=True)
+            nc.scalar.activation(out=smean[:, cols], in_=sm[:], func=ACT.Copy, scale=1.0 / N)
+
+        vmax = {}
+        vmin = {}
+        qsum = {}
+        zsum = {}
+        for fh in range(2):
+            vmax[fh] = const.tile([P, H], F32, name="vmax%d" % fh)
+            vmin[fh] = const.tile([P, H], F32, name="vmin%d" % fh)
+            qsum[fh] = const.tile([P, H], F32, name="qsum%d" % fh)
+            zsum[fh] = ps_sum.tile([P, H], F32, name="zsum%d" % fh)
+
+        def e_passes(dst, j, fh, first, last):
+            st, tl = j // JT, j % JT
+            cols = slice(H * fh, H * (fh + 1))
             for g in range(2):
+                one = slice((2 * tl + g) * P, (2 * tl + g + 1) * P)
+                nc.tensor.matmul_mx(
+                    out=dst[:],
+                    lhsT=ec[st][:, one].bitcast(X4),
+                    lhsT_scale=es[st][:, one],
+                    rhs=wc[4 + g][:, cols].bitcast(X4),
+                    rhs_scale=ws[4 + g][:, cols],
+                    start=(first and g == 0),
+                    stop=(last and g == 1),
+                )
+
+        def sum_passes(j, fh):
+            e_passes(zsum[fh], j, fh, j == 0, j == N - 1)
+
+        def open_bank(j, fh):
+            acc = ps_acc.tile([P, H], F32, name="acc", tag="acc")
+            e_passes(acc, j, fh, True, False)
+            return acc
+
+        def close_bank(acc, j, fh):
+            st, tl = j // JT, j % JT
+            cols = slice(H * fh, H * (fh + 1))
+            for g in range(2):
+                one = slice((2 * tl + g) * P, (2 * tl + g + 1) * P)
                 nc.tensor.matmul_mx(
                     out=acc[:],
-                    lhsT=wc[2 + g][:, cols].bitcast(X4),
-                    lhsT_scale=ws[2 + g][:, cols],
-                    rhs=xrc[b][:, g * 512 : (g + 1) * 512].bitcast(X4),
-                    rhs_scale=xrs[b][:, g * 512 : (g + 1) * 512],
+                    lhsT=xrc[st][:, one].bitcast(X4),
+                    lhsT_scale=xrs[st][:, one],
+                    rhs=wc[2 + g][:, cols].bitcast(X4),
+                    rhs_scale=ws[2 + g][:, cols],
                     start=False,
                     stop=(g == 1),
                 )
-            by_j = acc[:].rearrange("p (c j) -> p j c", j=N)
-            nc.scalar.copy(out=sq[rb][:, 1, :, 16 * ft : 16 * (ft + 1)], in_=by_j)
-            nc.scalar.activation(out=sq[rb][:, 0, :, 16 * ft : 16 * (ft + 1)], in_=by_j, func=ACT.Square)
+            if j == 0:
+                nc.scalar.copy(out=vmax[fh][:], in_=acc[:])
+                nc.scalar.activation(out=qsum[fh][:], in_=acc[:], func=ACT.Square)
+                return
+            if j == 1:
+                nc.vector.tensor_tensor(out=vmin[fh][:], in0=acc[:], in1=vmax[fh][:], op=ALU.min)
+            else:
+                nc.vector.tensor_tensor(out=vmin[fh][:], in0=acc[:], in1=vmin[fh][:], op=ALU.min)
+            nc.vector.tensor_tensor(out=vmax[fh][:], in0=acc[:], in1=vmax[fh][:], op=ALU.max)
+            sq = sqpool.tile([P, H], F32, name="sq", tag="sq")
+            nc.scalar.activation(out=sq[:], in_=acc[:], func=ACT.Square)
+            nc.gpsimd.tensor_tensor(out=qsum[fh][:], in0=qsum[fh][:], in1=sq[:], op=ALU.add)
 
-        def trees(rb, f0, f1):
-            b, h = rb // 2, rb % 2
-            c0 = 16 * h
-            cs = slice(16 * f0, 16 * f1)
-            z = sq[rb]
-            tmax = treepool.tile([P, 16, P], F32, name="tmax", tag="tmax")
-            tmin = treepool.tile([P, 16, P], F32, name="tmin", tag="tmin")
-            both = ((tmax, ALU.max, 2), (tmin, ALU.min, 1))
-            for t, op, a in both:
-                nc.vector.tensor_tensor(out=t[:, 0:16, cs], in0=z[:, 1, 0:16, cs], in1=z[:, 1, 16:32, cs], op=op)
-            for n in (8, 4, 2):
-                for t, op, a in both:
-                    nc.vector.tensor_tensor(out=t[:, 0:n, cs], in0=t[:, 0:n, cs], in1=t[:, n : 2 * n, cs], op=op)
-            for t, op, a in both:
-                nc.vector.tensor_tensor(
-                    out=res[b][:, f0:f1, a, c0 : c0 + 16],
-                    in0=t[:, 0, cs].rearrange("p (f c) -> p f c", c=16),
-                    in1=t[:, 1, cs].rearrange("p (f c) -> p f c", c=16),
-                    op=op,
-                )
+        def finish_minmax(fh):
+            cols = slice(H * fh, H * (fh + 1))
+            for a, v in ((1, vmin[fh]), (2, vmax[fh])):
+                res = const.tile([P, H], F32, name="res%d_%d" % (a, fh))
+                nc.vector.tensor_tensor(out=res[:], in0=v[:], in1=tb[:, cols], op=ALU.add)
+                nc.sync.dma_start(out=out_view[:, a, cols], in_=res[:])
 
-        def fold_squares(rb):
-            nc.vector.tensor_tensor(
-                out=sq[rb][:, 0, 0:16, :], in0=sq[rb][:, 0, 0:16, :], in1=sq[rb][:, 0, 16:32, :], op=ALU.add
-            )
-
-        sum_order = [(1, j, N) for j in range(N)] + [(0, j, N // 2) for j in range(N // 2)]
-
-        def sum_run(rb, part):
-            if part == 0:
-                sp[rb] = ps_sum.tile([P, 2, P], F32, name="sp", tag="sp")
-            for q, j, n in sum_order[12 * part : 12 * (part + 1)]:
-                nc.tensor.matmul(
-                    out=sp[rb][:, q, :], lhsT=sq[rb][:, q, j, :], rhs=ident[:], is_transpose=True,
-                    start=(j == 0), stop=(j == n - 1),
-                )
-
-        def sums_back(rb):
-            b, h = rb // 2, rb % 2
-            c0 = 16 * h
-            s2 = gpool.tile([P, 2, P], F32, name="s2", tag="s2")
-            nc.scalar.copy(out=s2[:], in_=sp[rb][:])
-            bk = ps_fin.tile([P, 2, P], F32, name="bk", tag="fin")
-            for q in range(2):
-                nc.tensor.transpose(bk[:, q, :], s2[:, q, :], ident[:])
-            s_z = bk[:, 1, :].rearrange("p (f c) -> p f c", c=16)
-            s_zz = bk[:, 0, :].rearrange("p (f c) -> p f c", c=16)
-            nc.scalar.activation(out=res[b][:, :, 0, c0 : c0 + 16], in_=s_z, func=ACT.Copy, scale=1.0 / N)
-            nc.scalar.activation(out=msq[b][:, :, c0 : c0 + 16], in_=s_z, func=ACT.Square, scale=1.0 / N)
+        def finish_sums(fh):
+            cols = slice(H * fh, H * (fh + 1))
+            mean = const.tile([P, H], F32, name="mean%d" % fh)
+            std = const.tile([P, H], F32, name="std%d" % fh)
+            mz = const.tile([P, H], F32, name="mz%d" % fh)
+            msq = const.tile([P, H], F32, name="msq%d" % fh)
+            var = const.tile([P, H], F32, name="var%d" % fh)
             nc.vector.scalar_tensor_tensor(
-                out=var[b][:, :, c0 : c0 + 16], in0=s_zz, scalar=1.0 / N, in1=msq[b][:, :, c0 : c0 + 16],
-                op0=ALU.mult, op1=ALU.subtract,
+                out=mz[:], in0=zsum[fh][:], scalar=1.0 / N, in1=smean[:, cols], op0=ALU.mult, op1=ALU.add
             )
+            nc.scalar.activation(out=msq[:], in_=mz[:], func=ACT.Square)
+            nc.gpsimd.tensor_tensor(out=mean[:], in0=mz[:], in1=tb[:, cols], op=ALU.add)
+            nc.sync.dma_start(out=out_view[:, 0, cols], in_=mean[:])
+            nc.vector.scalar_tensor_tensor(
+                out=var[:], in0=qsum[fh][:], scalar=1.0 / N, in1=msq[:], op0=ALU.mult, op1=ALU.subtract
+            )
+            nc.vector.tensor_scalar(out=var[:], in0=var[:], scalar1=0.0, scalar2=EPS_STD, op0=ALU.max, op1=ALU.add)
+            nc.scalar.activation(out=std[:], in_=var[:], func=ACT.Sqrt)
+            nc.sync.dma_start(out=out_view[:, 3, cols], in_=std[:])
 
-        def finish(b):
-            r = res[b]
-            nc.vector.tensor_scalar(
-                out=var[b][:], in0=var[b][:], scalar1=0.0, scalar2=EPS_STD, op0=ALU.max, op1=ALU.add
-            )
-            nc.scalar.activation(out=r[:, :, 3, :], in_=var[b][:], func=ACT.Sqrt)
-            nc.vector.tensor_tensor(
-                out=r[:, :, 0:3, :], in0=r[:, :, 0:3, :],
-                in1=tb[:, :, b * N : (b + 1) * N].unsqueeze(2).to_broadcast([P, 8, 3, N]), op=ALU.add,
-            )
-            o_sb = gpool.tile([P, F], F32, name="o_sb", tag="o_sb")
-            for q2 in range(2):
-                fin = ps_fin.tile([P, 4, P], F32, name="fin", tag="fin")
-                for q in range(4):
-                    nc.tensor.transpose(fin[:, q, :], r[:, 4 * q2 + q, :, :].rearrange("p a c -> p (a c)"), ident[:])
-                nc.scalar.copy(out=o_sb[:, 512 * q2 : 512 * (q2 + 1)], in_=fin[:].rearrange("p q f -> p (q f)"))
-            for a in range(4):
-                nc.sync.dma_start(out=out[b, :, a * F : (a + 1) * F], in_=o_sb[a * N : (a + 1) * N, :])
+        def ahead(st, slot):
+            if slot == 0 and st + 3 < NSTEP:
+                load_e(st + 3)
+            if st + 1 < NSTEP:
+                if slot < JT:
+                    widen(st + 1, slot)
+                if slot == 1:
+                    rep_x(st + 1)
+                if slot in (2, 4):
+                    turn(st + 1, slot - 2)
+                    turn(st + 1, slot - 1)
+                if slot == 5:
+                    quant_e(st + 1, 0, JT)
+            if st == 1 and slot == 0:
+                nc.scalar.dma_start(out=bias_bc[:], in_=b_pre.partition_broadcast(P))
+            if st == 1 and slot in (5, 7):
+                source_mean((slot - 5) // 2)
+            if st == 4 and slot == 0:
+                for s, f2 in W_LATE:
+                    load_w(s, f2)
+            if st == 5 and slot >= JT:
+                s, f2 = W_LATE[slot - JT]
+                prep_w(s, f2, 0, 0)
+            if st == 6 and slot in (5, 7):
+                target_term((slot - 5) // 2)
 
-        widen(0)
+        widen(0, 0)
+        widen(0, 1)
         rep_x(0)
         turn(0, 0)
         turn(0, 1)
-        for s, fh in W_URGENT[0:2]:
-            prep_w(s, fh, CV)
-        quant_e(0)
-        for s, fh in W_URGENT[2:4]:
-            prep_w(s, fh, CV)
+        prep_w(4, 0, CV, 0)
+        prep_w(5, 0, CV, 0)
+        quant_e(0, 0, 2)
+        widen(0, 2)
+        widen(0, 3)
+        turn(0, 2)
+        turn(0, 3)
+        prep_w(2, 0, 0, CG)
+        quant_e(0, 2, 4)
+        prep_w(3, 0, 0, CG)
+        first = {}
+        for tl in range(JT):
+            sum_passes(tl, 0)
+            first[tl] = open_bank(tl, 0)
         for s, fh in W_URGENT[4:8]:
-            prep_w(s, fh, 0)
-        widen(1)
-        for rb in range(8):
-            b = rb // 2
-            if rb % 2 == 0:
-                res[b] = gpool.tile([P, 8, 4, N], F32, name="res%d" % b, tag="res")
-                var[b] = gpool.tile([P, 8, N], F32, name="var%d" % b, tag="var")
-                msq[b] = gpool.tile([P, 8, N], F32, name="msq%d" % b, tag="msq")
-            sq[rb] = sqpool.tile([P, 2, N, P], F32, name="sq%d" % rb, tag="sq")
-            if rb + 3 < 8:
-                load_e(rb + 3)
-            if rb == 0:
-                for s, fh in W_LATE:
-                    load_w(s, fh)
-            if rb + 2 < 8:
-                widen(rb + 2)
-            if rb >= 1:
-                fold_squares(rb - 1)
-                trees(rb - 1, 0, 8)
-            for half in range(2):
-                if rb + 1 < 8:
-                    turn(rb + 1, half)
-                for pair in range(2):
-                    if rb >= 1:
-                        sum_run(rb - 1, 2 * half + pair)
-                    bank(rb, 4 * half + 2 * pair)
-                    bank(rb, 4 * half + 2 * pair + 1)
-                if rb == 7:
-                    if half == 1:
-                        fold_squares(rb)
-                    trees(rb, 4 * half, 4 * half + 4)
-            if rb + 1 < 8:
-                quant_e(rb + 1)
-            if rb >= 1:
-                sums_back(rb - 1)
-                if rb % 2 == 0:
-                    finish(b - 1)
-            if rb < 2:
-                for s, fh in W_LATE[2 * rb : 2 * rb + 2]:
-                    prep_w(s, fh, 0)
-            if rb == 1:
-                target_term()
-            if rb % 2 == 0 and b + 1 < B:
-                rep_x(b + 1)
-        for part in range(4):
-            sum_run(7, part)
-        sums_back(7)
-        finish(3)
+            prep_w(s, fh, 0, CG)
+        for st in range(NSTEP):
+            for fh in range(2):
+                for tl in range(JT):
+                    j = JT * st + tl
+                    ahead(st, JT * fh + tl)
+                    if st == 0 and fh == 0:
+                        close_bank(first[tl], j, fh)
+                        continue
+                    if st < NSTEP - 1:
+                        sum_passes(j, fh)
+                    close_bank(open_bank(j, fh), j, fh)
+                if st == NSTEP - 1:
+                    finish_minmax(fh)
+        for fh in range(2):
+            for tl in range(JT):
+                sum_passes(JT * (NSTEP - 1) + tl, fh)
+            finish_sums(fh)

@@ -112,28 +112,34 @@ def tile_gnnlayer_pa_kernel(tc, x, e_enc_bytes, e_enc_scale, W_pre, b_pre, out):
         xs = const.tile([P, 2 * P], U8, name="xs", align_bytes=64)
         nc.vector.memset(xs[:].bitcast(I32), 0)
         nc.vector.quantize_mx(out=xc[:].bitcast(X4), scales=xs[:], in_=xg[:])
-        xs4 = const.tile([P, 4 * 2 * P], U8, name="xs4", align_bytes=64)
-        for r in range(4):
-            nc.vector.tensor_copy(out=xs4[:].rearrange("p (c r) -> p c r", r=4)[:, :, r], in_=xs[:])
+        xj = const.tile([P, 2 * P * 2], F32, name="xj")
+        nc.scalar.copy(
+            out=xj[:].rearrange("p (g j b u) -> p g j b u", g=2, b=B, u=2)[:, 0],
+            in_=xt[:, 0:2, :].rearrange("p u (b j) -> p j b u", b=B),
+        )
+        nc.scalar.copy(
+            out=xj[:].rearrange("p (g j b u) -> p g j b u", g=2, b=B, u=2)[:, 1],
+            in_=xt[:, 2:4, :].rearrange("p u (b j) -> p j b u", b=B),
+        )
 
         xrc = {}
         xrs = {}
 
+        xrg = {}
+
         def rep_x(st):
-            xrc[st] = xrpool.tile([P, JT * 2 * P], U32, name="xrc%d" % st, tag="xrc", align_bytes=64)
-            xrs[st] = xrpool.tile([P, JT * 2 * P], U8, name="xrs%d" % st, tag="xrs", align_bytes=64)
-            js = slice(JT * st, JT * (st + 1))
+            xrg[st] = xrpool.tile([P, 2 * JT * P * 4], BF16, name="xrg%d" % st, tag="xrg", align_bytes=64)
             for g in range(2):
-                one = slice(g * P, (g + 1) * P)
-                nc.gpsimd.tensor_copy(
-                    out=xrc[st][:].rearrange("p (t g b i) -> p t g b i", t=JT, g=2, b=B)[:, :, g],
-                    in_=xc[:, one].rearrange("p (b j) -> p j b", b=B)[:, js, :].unsqueeze(3).to_broadcast([P, JT, B, N]),
+                nc.scalar.copy(
+                    out=xrg[st][:].bitcast(F32).rearrange("p (g c i u) -> p g c i u", g=2, i=N, u=2)[:, g],
+                    in_=xj[:].rearrange("p (g c u) -> p g c u", g=2, u=2)[:, g, JT * B * st : JT * B * (st + 1), :]
+                    .unsqueeze(2).to_broadcast([P, JT * B, N, 2]),
                 )
-                nc.gpsimd.tensor_copy(
-                    out=xrs[st][:].bitcast(U32).rearrange("p (t g b w) -> p t g b w", t=JT, g=2, b=B)[:, :, g],
-                    in_=xs4[:].bitcast(U32)[:, one].rearrange("p (b j) -> p j b", b=B)[:, js, :]
-                    .unsqueeze(3).to_broadcast([P, JT, B, N // 4]),
-                )
+
+        def quant_x(st):
+            xrc[st] = xrpool.tile([P, 2 * JT * P], U32, name="xrc%d" % st, tag="xrc", align_bytes=64)
+            xrs[st] = xrpool.tile([P, 2 * JT * P], U8, name="xrs%d" % st, tag="xrs", align_bytes=64)
+            nc.vector.quantize_mx(out=xrc[st][:].bitcast(X4), scales=xrs[st][:], in_=xrg[st][:])
 
         ebf = {}
         eg = {}
@@ -236,7 +242,7 @@ def tile_gnnlayer_pa_kernel(tc, x, e_enc_bytes, e_enc_scale, W_pre, b_pre, out):
             st, tl = j // JT, j % JT
             cols = slice(H * fh, H * (fh + 1))
             for g in range(2):
-                one = slice((2 * tl + g) * P, (2 * tl + g + 1) * P)
+                one = slice((JT * g + tl) * P, (JT * g + tl + 1) * P)
                 nc.tensor.matmul_mx(
                     out=acc[:],
                     lhsT=xrc[st][:, one].bitcast(X4),
@@ -294,6 +300,8 @@ def tile_gnnlayer_pa_kernel(tc, x, e_enc_bytes, e_enc_scale, W_pre, b_pre, out):
                     widen(st + 1, slot)
                 if slot == 1:
                     rep_x(st + 1)
+                if slot == 6:
+                    quant_x(st + 1)
                 if slot in (2, 4):
                     turn(st + 1, slot - 2)
                     turn(st + 1, slot - 1)
@@ -324,15 +332,16 @@ def tile_gnnlayer_pa_kernel(tc, x, e_enc_bytes, e_enc_scale, W_pre, b_pre, out):
         widen(0, 3)
         turn(0, 2)
         turn(0, 3)
-        prep_w(2, 0, 0, CG)
+        quant_x(0)
+        prep_w(2, 0, CV, 0)
         quant_e(0, 2, 4)
-        prep_w(3, 0, 0, CG)
+        prep_w(3, 0, CV, 0)
         first = {}
         for tl in range(JT):
             sum_passes(tl, 0)
             first[tl] = open_bank(tl, 0)
         for s, fh in W_URGENT[4:8]:
-            prep_w(s, fh, 0, CG)
+            prep_w(s, fh, 0, 0)
         for st in range(NSTEP):
             for fh in range(2):
                 for tl in range(JT):

@@ -51,8 +51,11 @@ def tile_gnnlayer_pa_kernel(tc, x, e_enc_bytes, e_enc_scale, W_pre, b_pre, out):
         make_identity(nc, ident[:])
         blk = const.tile([P, P], F32, name="blk")
         make_block_diagonal(nc, blk[:], N)
-        scl = const.tile([P, C], F32, name="scl")
-        nc.scalar.dma_start(out=scl[:], in_=e_enc_scale.rearrange("a b c k -> (a b c k)").partition_broadcast(P))
+        scl = const.tile([P, 2, 2, 2], F32, name="scl")
+        nc.scalar.dma_start(
+            out=scl[:].rearrange("p g u e -> p g (u e)"),
+            in_=e_enc_scale.rearrange("a b c (g p t) -> p (a b c g) t", p=P, t=4),
+        )
         warm = const.tile([P, 2], F32, name="warm")
         nc.vector.memset(warm[:], 1.0)
         nc.scalar.activation(out=warm[:, 1:2], in_=warm[:, 0:1], func=ACT.Sqrt)
@@ -149,20 +152,23 @@ def tile_gnnlayer_pa_kernel(tc, x, e_enc_bytes, e_enc_scale, W_pre, b_pre, out):
         def widen(st, tl):
             if tl == 0:
                 ebf[st] = ebfpool.tile([P, JT, C], BF16, name="ebf%d" % st, tag="ebf")
-            nc.vector.tensor_tensor(
-                out=ebf[st][:, tl, :], in0=eb[st][:, tl, :].bitcast(FP8), in1=scl[:], op=ALU.mult
-            )
+            nc.scalar.copy(out=ebf[st][:, tl, :], in_=eb[st][:, tl, :].bitcast(FP8))
 
         def turn(st, tl):
             if tl == 0:
                 eg[st] = egpool.tile([P, JT * 2 * P * 4], BF16, name="eg%d" % st, tag="eg", align_bytes=64)
-            eg_w = eg[st][:].bitcast(F32).rearrange("p (t g r u) -> p t g r u", t=JT, g=2, u=2)
+            eg_v = eg[st][:].rearrange("p (t g r u e) -> p t g r u e", t=JT, g=2, u=2, e=2)
             words = ebf[st][:, tl, :].bitcast(F32)
             tp = ps_tp.tile([P, 2, 2, P], F32, name="tp", tag="tp")
             for g in range(2):
                 for u in range(2):
                     nc.tensor.transpose(tp[:, g, u, :], words[:, 256 * g + u : 256 * (g + 1) : 2], ident[:])
-            nc.scalar.copy(out=eg_w[:, tl], in_=tp[:].rearrange("p g u r -> p g r u"))
+            pairs = tp[:].bitcast(BF16).rearrange("p g u (r e) -> p g r u e", e=2)
+            for g in range(2):
+                nc.vector.tensor_tensor(
+                    out=eg_v[:, tl, g], in0=pairs[:, g], in1=scl[:, g].unsqueeze(1).to_broadcast([P, P, 2, 2]),
+                    op=ALU.mult,
+                )
 
         def quant_e(st, t0, t1):
             if t0 == 0:

@@ -56,6 +56,12 @@ def tile_gnnlayer_pa_kernel(tc, x, e_enc_bytes, e_enc_scale, W_pre, b_pre, out):
             out=scl[:].rearrange("p g u e -> p g (u e)"),
             in_=e_enc_scale.rearrange("a b c (g p t) -> p (a b c g) t", p=P, t=4),
         )
+        sclr = const.tile([P, 2, P, 4], F32, name="sclr")
+        for g in range(2):
+            nc.gpsimd.tensor_copy(
+                out=sclr[:, g], in_=scl[:, g].rearrange("p u e -> p (u e)").unsqueeze(1).to_broadcast([P, P, 4])
+            )
+        sclrow = const.tile([P, C], F32, name="sclrow")
         warm = const.tile([P, 2], F32, name="warm")
         nc.vector.memset(warm[:], 1.0)
         nc.scalar.activation(out=warm[:, 1:2], in_=warm[:, 0:1], func=ACT.Sqrt)
@@ -78,6 +84,7 @@ def tile_gnnlayer_pa_kernel(tc, x, e_enc_bytes, e_enc_scale, W_pre, b_pre, out):
         for s, fh in W_URGENT[0:4]:
             load_w(s, fh)
         load_e(1)
+        nc.sync.dma_start(out=sclrow[:], in_=e_enc_scale.rearrange("a b c k -> (a b c k)").partition_broadcast(P))
         for s, fh in W_URGENT[4:8]:
             load_w(s, fh)
         load_e(2)
@@ -115,58 +122,61 @@ def tile_gnnlayer_pa_kernel(tc, x, e_enc_bytes, e_enc_scale, W_pre, b_pre, out):
         xs = const.tile([P, 2 * P], U8, name="xs", align_bytes=64)
         nc.vector.memset(xs[:].bitcast(I32), 0)
         nc.vector.quantize_mx(out=xc[:].bitcast(X4), scales=xs[:], in_=xg[:])
-        xj = const.tile([P, 2 * P * 2], F32, name="xj")
-        nc.scalar.copy(
-            out=xj[:].rearrange("p (g j b u) -> p g j b u", g=2, b=B, u=2)[:, 0],
-            in_=xt[:, 0:2, :].rearrange("p u (b j) -> p j b u", b=B),
-        )
-        nc.scalar.copy(
-            out=xj[:].rearrange("p (g j b u) -> p g j b u", g=2, b=B, u=2)[:, 1],
-            in_=xt[:, 2:4, :].rearrange("p u (b j) -> p j b u", b=B),
-        )
+        xs4 = const.tile([P, 4 * 2 * P], U8, name="xs4", align_bytes=64)
+        for r in range(4):
+            nc.vector.tensor_copy(out=xs4[:].rearrange("p (c r) -> p c r", r=4)[:, :, r], in_=xs[:])
 
         xrc = {}
         xrs = {}
 
-        xrg = {}
-
         def rep_x(st):
-            xrg[st] = xrpool.tile([P, 2 * JT * P * 4], BF16, name="xrg%d" % st, tag="xrg", align_bytes=64)
+            xrc[st] = xrpool.tile([P, JT * 2 * P], U32, name="xrc%d" % st, tag="xrc", align_bytes=64)
+            xrs[st] = xrpool.tile([P, JT * 2 * P], U8, name="xrs%d" % st, tag="xrs", align_bytes=64)
+            js = slice(JT * st, JT * (st + 1))
             for g in range(2):
-                nc.scalar.copy(
-                    out=xrg[st][:].bitcast(F32).rearrange("p (g c i u) -> p g c i u", g=2, i=N, u=2)[:, g],
-                    in_=xj[:].rearrange("p (g c u) -> p g c u", g=2, u=2)[:, g, JT * B * st : JT * B * (st + 1), :]
-                    .unsqueeze(2).to_broadcast([P, JT * B, N, 2]),
+                one = slice(g * P, (g + 1) * P)
+                nc.gpsimd.tensor_copy(
+                    out=xrc[st][:].rearrange("p (t g b i) -> p t g b i", t=JT, g=2, b=B)[:, :, g],
+                    in_=xc[:, one].rearrange("p (b j) -> p j b", b=B)[:, js, :].unsqueeze(3).to_broadcast([P, JT, B, N]),
                 )
-
-        def quant_x(st):
-            xrc[st] = xrpool.tile([P, 2 * JT * P], U32, name="xrc%d" % st, tag="xrc", align_bytes=64)
-            xrs[st] = xrpool.tile([P, 2 * JT * P], U8, name="xrs%d" % st, tag="xrs", align_bytes=64)
-            nc.vector.quantize_mx(out=xrc[st][:].bitcast(X4), scales=xrs[st][:], in_=xrg[st][:])
+                nc.gpsimd.tensor_copy(
+                    out=xrs[st][:].bitcast(U32).rearrange("p (t g b w) -> p t g b w", t=JT, g=2, b=B)[:, :, g],
+                    in_=xs4[:].bitcast(U32)[:, one].rearrange("p (b j) -> p j b", b=B)[:, js, :]
+                    .unsqueeze(3).to_broadcast([P, JT, B, N // 4]),
+                )
 
         ebf = {}
         eg = {}
         ec = {}
         es = {}
 
+        def by_gpsimd(st, tl):
+            return st > 0 and tl == 0
+
         def widen(st, tl):
             if tl == 0:
                 ebf[st] = ebfpool.tile([P, JT, C], BF16, name="ebf%d" % st, tag="ebf")
             nc.scalar.copy(out=ebf[st][:, tl, :], in_=eb[st][:, tl, :].bitcast(FP8))
+            if by_gpsimd(st, tl):
+                nc.gpsimd.tensor_tensor(out=ebf[st][:, tl, :], in0=ebf[st][:, tl, :], in1=sclrow[:], op=ALU.mult)
 
         def turn(st, tl):
-            if tl == 0:
+            if st not in eg:
                 eg[st] = egpool.tile([P, JT * 2 * P * 4], BF16, name="eg%d" % st, tag="eg", align_bytes=64)
-            eg_v = eg[st][:].rearrange("p (t g r u e) -> p t g r u e", t=JT, g=2, u=2, e=2)
+            eg_v = eg[st][:].rearrange("p (t c u e) -> p t c u e", t=JT, u=2, e=2)
+            eg_w = eg[st][:].bitcast(F32).rearrange("p (t c u) -> p t c u", t=JT, u=2)
             words = ebf[st][:, tl, :].bitcast(F32)
             tp = ps_tp.tile([P, 2, 2, P], F32, name="tp", tag="tp")
             for g in range(2):
                 for u in range(2):
-                    nc.tensor.transpose(tp[:, g, u, :], words[:, 256 * g + u : 256 * (g + 1) : 2], ident[:])
-            pairs = tp[:].bitcast(BF16).rearrange("p g u (r e) -> p g r u e", e=2)
-            for g in range(2):
+                    nc.tensor.transpose(tp[:, u, g, :], words[:, 256 * g + u : 256 * (g + 1) : 2], ident[:])
+            if by_gpsimd(st, tl):
+                nc.scalar.copy(out=eg_w[:, tl], in_=tp[:].rearrange("p u g r -> p (g r) u"))
+            else:
                 nc.vector.tensor_tensor(
-                    out=eg_v[:, tl, g], in0=pairs[:, g], in1=scl[:, g].unsqueeze(1).to_broadcast([P, P, 2, 2]),
+                    out=eg_v[:, tl],
+                    in0=tp[:].bitcast(BF16).rearrange("p u g (r e) -> p (g r) u e", e=2),
+                    in1=sclr[:].rearrange("p g r (u e) -> p (g r) u e", e=2),
                     op=ALU.mult,
                 )
 
@@ -248,7 +258,7 @@ def tile_gnnlayer_pa_kernel(tc, x, e_enc_bytes, e_enc_scale, W_pre, b_pre, out):
             st, tl = j // JT, j % JT
             cols = slice(H * fh, H * (fh + 1))
             for g in range(2):
-                one = slice((JT * g + tl) * P, (JT * g + tl + 1) * P)
+                one = slice((2 * tl + g) * P, (2 * tl + g + 1) * P)
                 nc.tensor.matmul_mx(
                     out=acc[:],
                     lhsT=xrc[st][:, one].bitcast(X4),
@@ -306,11 +316,12 @@ def tile_gnnlayer_pa_kernel(tc, x, e_enc_bytes, e_enc_scale, W_pre, b_pre, out):
                     widen(st + 1, slot)
                 if slot == 1:
                     rep_x(st + 1)
-                if slot == 6:
-                    quant_x(st + 1)
-                if slot in (2, 4):
-                    turn(st + 1, slot - 2)
-                    turn(st + 1, slot - 1)
+                if slot == 2:
+                    turn(st + 1, 1)
+                    turn(st + 1, 2)
+                if slot == 4:
+                    turn(st + 1, 3)
+                    turn(st + 1, 0)
                 if slot == 5:
                     quant_e(st + 1, 0, JT)
             if st == 1 and slot == 0:
@@ -338,7 +349,6 @@ def tile_gnnlayer_pa_kernel(tc, x, e_enc_bytes, e_enc_scale, W_pre, b_pre, out):
         widen(0, 3)
         turn(0, 2)
         turn(0, 3)
-        quant_x(0)
         prep_w(2, 0, CV, 0)
         quant_e(0, 2, 4)
         prep_w(3, 0, CV, 0)

@@ -42,7 +42,7 @@ def tile_gnnlayer_pa_kernel(tc, x, e_enc_bytes, e_enc_scale, W_pre, b_pre, out):
         egpool = ctx.enter_context(tc.tile_pool(name="egpool", bufs=2))
         ecpool = ctx.enter_context(tc.tile_pool(name="ecpool", bufs=2))
         xrpool = ctx.enter_context(tc.tile_pool(name="xrpool", bufs=2))
-        sqpool = ctx.enter_context(tc.tile_pool(name="sqpool", bufs=4))
+        sqpool = ctx.enter_context(tc.tile_pool(name="sqpool", bufs=6))
         ps_tp = ctx.enter_context(tc.psum_pool(name="ps_tp", bufs=2))
         ps_acc = ctx.enter_context(tc.psum_pool(name="ps_acc", bufs=4))
         ps_sum = ctx.enter_context(tc.psum_pool(name="ps_sum", bufs=1))
@@ -133,17 +133,15 @@ def tile_gnnlayer_pa_kernel(tc, x, e_enc_bytes, e_enc_scale, W_pre, b_pre, out):
             xrc[st] = xrpool.tile([P, JT * 2 * P], U32, name="xrc%d" % st, tag="xrc", align_bytes=64)
             xrs[st] = xrpool.tile([P, JT * 2 * P], U8, name="xrs%d" % st, tag="xrs", align_bytes=64)
             js = slice(JT * st, JT * (st + 1))
-            for g in range(2):
-                one = slice(g * P, (g + 1) * P)
-                nc.gpsimd.tensor_copy(
-                    out=xrc[st][:].rearrange("p (t g b i) -> p t g b i", t=JT, g=2, b=B)[:, :, g],
-                    in_=xc[:, one].rearrange("p (b j) -> p j b", b=B)[:, js, :].unsqueeze(3).to_broadcast([P, JT, B, N]),
-                )
-                nc.gpsimd.tensor_copy(
-                    out=xrs[st][:].bitcast(U32).rearrange("p (t g b w) -> p t g b w", t=JT, g=2, b=B)[:, :, g],
-                    in_=xs4[:].bitcast(U32)[:, one].rearrange("p (b j) -> p j b", b=B)[:, js, :]
-                    .unsqueeze(3).to_broadcast([P, JT, B, N // 4]),
-                )
+            nc.gpsimd.tensor_copy(
+                out=xrc[st][:].rearrange("p (t c i) -> p t c i", t=JT, i=N),
+                in_=xc[:].rearrange("p (c j) -> p j c", j=N)[:, js, :].unsqueeze(3).to_broadcast([P, JT, 2 * B, N]),
+            )
+            nc.gpsimd.tensor_copy(
+                out=xrs[st][:].bitcast(U32).rearrange("p (t c w) -> p t c w", t=JT, w=N // 4),
+                in_=xs4[:].bitcast(U32).rearrange("p (c j) -> p j c", j=N)[:, js, :]
+                .unsqueeze(3).to_broadcast([P, JT, 2 * B, N // 4]),
+            )
 
         ebf = {}
         eg = {}
@@ -228,8 +226,10 @@ def tile_gnnlayer_pa_kernel(tc, x, e_enc_bytes, e_enc_scale, W_pre, b_pre, out):
         for fh in range(2):
             vmax[fh] = const.tile([P, H], F32, name="vmax%d" % fh)
             vmin[fh] = const.tile([P, H], F32, name="vmin%d" % fh)
-            qsum[fh] = const.tile([P, H], F32, name="qsum%d" % fh)
+            qsum[fh] = const.tile([P, 2, H], F32, name="qsum%d" % fh)
             zsum[fh] = ps_sum.tile([P, H], F32, name="zsum%d" % fh)
+
+        sqs = {}
 
         def e_passes(dst, j, fh, first, last):
             st, tl = j // JT, j % JT
@@ -270,16 +270,21 @@ def tile_gnnlayer_pa_kernel(tc, x, e_enc_bytes, e_enc_scale, W_pre, b_pre, out):
                 )
             if j == 0:
                 nc.scalar.copy(out=vmax[fh][:], in_=acc[:])
-                nc.scalar.activation(out=qsum[fh][:], in_=acc[:], func=ACT.Square)
+                nc.scalar.activation(out=qsum[fh][:, 0, :], in_=acc[:], func=ACT.Square)
                 return
             if j == 1:
                 nc.vector.tensor_tensor(out=vmin[fh][:], in0=acc[:], in1=vmax[fh][:], op=ALU.min)
             else:
                 nc.vector.tensor_tensor(out=vmin[fh][:], in0=acc[:], in1=vmin[fh][:], op=ALU.min)
             nc.vector.tensor_tensor(out=vmax[fh][:], in0=acc[:], in1=vmax[fh][:], op=ALU.max)
-            sq = sqpool.tile([P, H], F32, name="sq", tag="sq")
-            nc.scalar.activation(out=sq[:], in_=acc[:], func=ACT.Square)
-            nc.gpsimd.tensor_tensor(out=qsum[fh][:], in0=qsum[fh][:], in1=sq[:], op=ALU.add)
+            if j == 1:
+                nc.scalar.activation(out=qsum[fh][:, 1, :], in_=acc[:], func=ACT.Square)
+                return
+            if j % 2 == 0:
+                sqs[fh] = sqpool.tile([P, 2, H], F32, name="sq", tag="sq")
+            nc.scalar.activation(out=sqs[fh][:, j % 2, :], in_=acc[:], func=ACT.Square)
+            if j % 2 == 1:
+                nc.gpsimd.tensor_tensor(out=qsum[fh][:], in0=qsum[fh][:], in1=sqs[fh][:], op=ALU.add)
 
         def finish_minmax(fh):
             cols = slice(H * fh, H * (fh + 1))
@@ -302,7 +307,10 @@ def tile_gnnlayer_pa_kernel(tc, x, e_enc_bytes, e_enc_scale, W_pre, b_pre, out):
             nc.gpsimd.tensor_tensor(out=mean[:], in0=mz[:], in1=tb[:, cols], op=ALU.add)
             nc.sync.dma_start(out=out_view[:, 0, cols], in_=mean[:])
             nc.vector.scalar_tensor_tensor(
-                out=var[:], in0=qsum[fh][:], scalar=1.0 / N, in1=msq[:], op0=ALU.mult, op1=ALU.subtract
+                out=var[:], in0=qsum[fh][:, 0, :], scalar=1.0 / N, in1=msq[:], op0=ALU.mult, op1=ALU.subtract
+            )
+            nc.vector.scalar_tensor_tensor(
+                out=var[:], in0=qsum[fh][:, 1, :], scalar=1.0 / N, in1=var[:], op0=ALU.mult, op1=ALU.add
             )
             nc.vector.tensor_scalar(out=var[:], in0=var[:], scalar1=0.0, scalar2=EPS_STD, op0=ALU.max, op1=ALU.add)
             nc.scalar.activation(out=std[:], in_=var[:], func=ACT.Sqrt)

@@ -95,7 +95,9 @@ def tile_gnnlayer_pa_kernel(tc, x, e_enc_bytes, e_enc_scale, W_pre, b_pre, out):
             wc[s] = const.tile([P, F], U32, name="wc%d" % s, align_bytes=64)
             ws[s] = const.tile([P, F], U8, name="ws%d" % s, align_bytes=64)
 
-        def prep_w(s, fh, cv, cg):
+        wgs = {}
+
+        def prep_w(s, fh, cv, cg, late=False):
             raw = wraw[(s, fh)]
             wg = wgpool.tile([P, H, 4], BF16, name="wg%d_%d" % (s, fh), tag="wg", align_bytes=64)
             if cv > 0:
@@ -105,9 +107,15 @@ def tile_gnnlayer_pa_kernel(tc, x, e_enc_bytes, e_enc_scale, W_pre, b_pre, out):
                     out=wg[:, cv : cv + cg, :], in_=raw[:, :, cv : cv + cg].rearrange("p t f -> p f t")
                 )
             nc.scalar.copy(out=wg[:, cv + cg : H, :], in_=raw[:, :, cv + cg : H].rearrange("p t f -> p f t"))
+            wgs[(s, fh)] = wg
+            if not late:
+                quant_w(s, fh)
+
+        def quant_w(s, fh):
             cols = slice(H * fh, H * (fh + 1))
             nc.vector.quantize_mx(
-                out=wc[s][:, cols].bitcast(X4), scales=ws[s][:, cols], in_=wg[:].rearrange("p f t -> p (f t)")
+                out=wc[s][:, cols].bitcast(X4), scales=ws[s][:, cols],
+                in_=wgs[(s, fh)][:].rearrange("p f t -> p (f t)"),
             )
 
         xw = x_sb[:].bitcast(F32)
@@ -330,18 +338,21 @@ def tile_gnnlayer_pa_kernel(tc, x, e_enc_bytes, e_enc_scale, W_pre, b_pre, out):
                 if slot == 4:
                     turn(st + 1, 3)
                     turn(st + 1, 0)
-                if slot == 5:
+                if slot == 6:
                     quant_e(st + 1, 0, JT)
             if st == 1 and slot == 0:
                 nc.scalar.dma_start(out=bias_bc[:], in_=b_pre.partition_broadcast(P))
             if st == 1 and slot in (5, 7):
                 source_mean((slot - 5) // 2)
-            if st == 4 and slot == 0:
+            if st == 3 and slot == 0:
                 for s, f2 in W_LATE:
                     load_w(s, f2)
-            if st == 5 and slot >= JT:
-                s, f2 = W_LATE[slot - JT]
-                prep_w(s, f2, 0, 0)
+            if st in (4, 5) and slot in (0, 1):
+                s, f2 = W_LATE[2 * (st - 4) + slot]
+                prep_w(s, f2, 0, 0, late=True)
+            if st in (4, 5) and slot in (2, 4):
+                s, f2 = W_LATE[2 * (st - 4) + (slot - 2) // 2]
+                quant_w(s, f2)
             if st == 6 and slot in (5, 7):
                 target_term((slot - 5) // 2)
 

@@ -342,8 +342,8 @@ def tile_gnnlayer_pa_kernel(tc, x, e_enc_bytes, e_enc_scale, W_pre, b_pre, out):
                     quant_e(st + 1, 0, JT)
             if st == 1 and slot == 0:
                 nc.scalar.dma_start(out=bias_bc[:], in_=b_pre.partition_broadcast(P))
-            if st == 1 and slot in (5, 7):
-                source_mean((slot - 5) // 2)
+            if st == 0 and slot in (3, 7):
+                source_mean((slot - 3) // 4)
             if st == 3 and slot == 0:
                 for s, f2 in W_LATE:
                     load_w(s, f2)

from contextlib import ExitStack

import concourse.mybir as mybir
from concourse.masks import make_block_diagonal, make_identity

B, N, C, F = 4, 32, 1024, 1024
EPS_STD = 1e-5
FLOPS = 2 * (B * N * N + 2 * B * N) * C * F

F32 = mybir.dt.float32
BF16 = mybir.dt.bfloat16
U32 = mybir.dt.uint32
I32 = mybir.dt.int32
U8 = mybir.dt.uint8
FP8 = mybir.dt.float8_e4m3fn
X4 = mybir.dt.float8_e4m3fn_x4
ALU = mybir.AluOpType
ACT = mybir.ActivationFunctionType

P = 128
H = 512
JT = 4
NSTEP = N // JT
CV = 336
CG = 128
W_URGENT = ((4, 0), (5, 0), (2, 0), (3, 0), (4, 1), (5, 1), (2, 1), (3, 1))
W_LATE = ((0, 0), (1, 0), (0, 1), (1, 1))


def tile_gnnlayer_pa_kernel(tc, x, e_enc_bytes, e_enc_scale, W_pre, b_pre, out):
    nc = tc.nc
    e_view = e_enc_bytes.rearrange("b i (n t) k -> n (b i) t k", t=JT)
    w_view = W_pre.rearrange("(s p t) f -> s p t f", p=P, t=4)
    out_view = out.rearrange("b i (a f) -> (b i) a f", a=4)

    with ExitStack() as ctx:
        const = ctx.enter_context(tc.tile_pool(name="const", bufs=1))
        wstage = ctx.enter_context(tc.tile_pool(name="wstage", bufs=4))
        wgpool = ctx.enter_context(tc.tile_pool(name="wgpool", bufs=2))
        ebpool = ctx.enter_context(tc.tile_pool(name="ebpool", bufs=3))
        ebfpool = ctx.enter_context(tc.tile_pool(name="ebfpool", bufs=2))
        egpool = ctx.enter_context(tc.tile_pool(name="egpool", bufs=2))
        ecpool = ctx.enter_context(tc.tile_pool(name="ecpool", bufs=2))
        xrpool = ctx.enter_context(tc.tile_pool(name="xrpool", bufs=2))
        sqpool = ctx.enter_context(tc.tile_pool(name="sqpool", bufs=6))
        ps_tp = ctx.enter_context(tc.psum_pool(name="ps_tp", bufs=2))
        ps_acc = ctx.enter_context(tc.psum_pool(name="ps_acc", bufs=4))
        ps_sum = ctx.enter_context(tc.psum_pool(name="ps_sum", bufs=1))

        ident = const.tile([P, P], F32, name="ident")
        make_identity(nc, ident[:])
        blk = const.tile([P, P], F32, name="blk")
        make_block_diagonal(nc, blk[:], N)
        scl = const.tile([P, 2, 2, 2], F32, name="scl")
        nc.scalar.dma_start(
            out=scl[:].rearrange("p g u e -> p g (u e)"),
            in_=e_enc_scale.rearrange("a b c (g p t) -> p (a b c g) t", p=P, t=4),
        )
        sclr = const.tile([P, 2, P, 4], F32, name="sclr")
        for g in range(2):
            nc.gpsimd.tensor_copy(
                out=sclr[:, g], in_=scl[:, g].rearrange("p u e -> p (u e)").unsqueeze(1).to_broadcast([P, P, 4])
            )
        sclrow = const.tile([P, C], F32, name="sclrow")
        warm = const.tile([P, 2], F32, name="warm")
        nc.vector.memset(warm[:], 1.0)
        nc.scalar.activation(out=warm[:, 1:2], in_=warm[:, 0:1], func=ACT.Sqrt)
        x_sb = const.tile([P, C], BF16, name="x_sb")
        nc.sync.dma_start(out=x_sb[:], in_=x.rearrange("b n c -> (b n) c"))
        bias_bc = const.tile([P, F], BF16, name="bias_bc")

        eb = {}
        wraw = {}

        def load_e(st):
            eb[st] = ebpool.tile([P, JT, C], U8, name="ebytes%d" % st, tag="ebytes")
            nc.sync.dma_start(out=eb[st][:], in_=e_view[st])

        def load_w(s, fh):
            wraw[(s, fh)] = wstage.tile([P, 4, H], BF16, name="wraw%d_%d" % (s, fh), tag="wraw")
            nc.sync.dma_start(out=wraw[(s, fh)][:], in_=w_view[s][:, :, H * fh : H * (fh + 1)])

        load_e(0)
        for s, fh in W_URGENT[0:4]:
            load_w(s, fh)
        load_e(1)
        nc.sync.dma_start(out=sclrow[:], in_=e_enc_scale.rearrange("a b c k -> (a b c k)").partition_broadcast(P))
        for s, fh in W_URGENT[4:8]:
            load_w(s, fh)
        load_e(2)

        wc = {}
        ws = {}
        for s in range(6):
            wc[s] = const.tile([P, F], U32, name="wc%d" % s, align_bytes=64)
            ws[s] = const.tile([P, F], U8, name="ws%d" % s, align_bytes=64)

        wgs = {}

        def prep_w(s, fh, cv, cg, late=False):
            raw = wraw[(s, fh)]
            wg = wgpool.tile([P, H, 4], BF16, name="wg%d_%d" % (s, fh), tag="wg", align_bytes=64)
            if cv > 0:
                nc.vector.tensor_copy(out=wg[:, 0:cv, :], in_=raw[:, :, 0:cv].rearrange("p t f -> p f t"))
            if cg > 0:
                nc.gpsimd.tensor_copy(
                    out=wg[:, cv : cv + cg, :], in_=raw[:, :, cv : cv + cg].rearrange("p t f -> p f t")
                )
            nc.scalar.copy(out=wg[:, cv + cg : H, :], in_=raw[:, :, cv + cg : H].rearrange("p t f -> p f t"))
            wgs[(s, fh)] = wg
            if not late:
                quant_w(s, fh)

        def quant_w(s, fh):
            cols = slice(H * fh, H * (fh + 1))
            nc.vector.quantize_mx(
                out=wc[s][:, cols].bitcast(X4), scales=ws[s][:, cols],
                in_=wgs[(s, fh)][:].rearrange("p f t -> p (f t)"),
            )

        xw = x_sb[:].bitcast(F32)
        xt = ps_tp.tile([P, 4, P], F32, name="xt", tag="tp")
        for g in range(2):
            for u in range(2):
                nc.tensor.transpose(xt[:, 2 * g + u, :], xw[:, 256 * g + u : 256 * (g + 1) : 2], ident[:])
        xg = const.tile([P, 2 * P * 4], BF16, name="xg", align_bytes=64)
        xg_w = xg[:].bitcast(F32).rearrange("p (g r u) -> p g r u", g=2, u=2)
        nc.scalar.copy(out=xg_w, in_=xt[:].rearrange("p (g u) r -> p g r u", u=2))
        xc = const.tile([P, 2 * P], U32, name="xc", align_bytes=64)
        xs = const.tile([P, 2 * P], U8, name="xs", align_bytes=64)
        nc.vector.memset(xs[:].bitcast(I32), 0)
        nc.vector.quantize_mx(out=xc[:].bitcast(X4), scales=xs[:], in_=xg[:])
        xs4 = const.tile([P, 4 * 2 * P], U8, name="xs4", align_bytes=64)
        for r in range(4):
            nc.vector.tensor_copy(out=xs4[:].rearrange("p (c r) -> p c r", r=4)[:, :, r], in_=xs[:])

        xrc = {}
        xrs = {}

        def rep_x(st):
            xrc[st] = xrpool.tile([P, JT * 2 * P], U32, name="xrc%d" % st, tag="xrc", align_bytes=64)
            xrs[st] = xrpool.tile([P, JT * 2 * P], U8, name="xrs%d" % st, tag="xrs", align_bytes=64)
            js = slice(JT * st, JT * (st + 1))
            nc.gpsimd.tensor_copy(
                out=xrc[st][:].rearrange("p (t c i) -> p t c i", t=JT, i=N),
                in_=xc[:].rearrange("p (c j) -> p j c", j=N)[:, js, :].unsqueeze(3).to_broadcast([P, JT, 2 * B, N]),
            )
            nc.gpsimd.tensor_copy(
                out=xrs[st][:].bitcast(U32).rearrange("p (t c w) -> p t c w", t=JT, w=N // 4),
                in_=xs4[:].bitcast(U32).rearrange("p (c j) -> p j c", j=N)[:, js, :]
                .unsqueeze(3).to_broadcast([P, JT, 2 * B, N // 4]),
            )

        ebf = {}
        eg = {}
        ec = {}
        es = {}

        def by_gpsimd(st, tl):
            return st > 0 and tl == 0

        def widen(st, tl):
            if tl == 0:
                ebf[st] = ebfpool.tile([P, JT, C], BF16, name="ebf%d" % st, tag="ebf")
            nc.scalar.copy(out=ebf[st][:, tl, :], in_=eb[st][:, tl, :].bitcast(FP8))
            if by_gpsimd(st, tl):
                nc.gpsimd.tensor_tensor(out=ebf[st][:, tl, :], in0=ebf[st][:, tl, :], in1=sclrow[:], op=ALU.mult)

        def turn(st, tl):
            if st not in eg:
                eg[st] = egpool.tile([P, JT * 2 * P * 4], BF16, name="eg%d" % st, tag="eg", align_bytes=64)
            eg_v = eg[st][:].rearrange("p (t c u e) -> p t c u e", t=JT, u=2, e=2)
            eg_w = eg[st][:].bitcast(F32).rearrange("p (t c u) -> p t c u", t=JT, u=2)
            words = ebf[st][:, tl, :].bitcast(F32)
            tp = ps_tp.tile([P, 2, 2, P], F32, name="tp", tag="tp")
            for g in range(2):
                for u in range(2):
                    nc.tensor.transpose(tp[:, u, g, :], words[:, 256 * g + u : 256 * (g + 1) : 2], ident[:])
            if by_gpsimd(st, tl):
                nc.scalar.copy(out=eg_w[:, tl], in_=tp[:].rearrange("p u g r -> p (g r) u"))
            else:
                nc.vector.tensor_tensor(
                    out=eg_v[:, tl],
                    in0=tp[:].bitcast(BF16).rearrange("p u g (r e) -> p (g r) u e", e=2),
                    in1=sclr[:].rearrange("p g r (u e) -> p (g r) u e", e=2),
                    op=ALU.mult,
                )

        def quant_e(st, t0, t1):
            if t0 == 0:
                ec[st] = ecpool.tile([P, JT * 2 * P], U32, name="ec%d" % st, tag="ec", align_bytes=64)
                es[st] = ecpool.tile([P, JT * 2 * P], U8, name="es%d" % st, tag="es", align_bytes=64)
            cols = slice(t0 * 2 * P, t1 * 2 * P)
            nc.vector.quantize_mx(
                out=ec[st][:, cols].bitcast(X4), scales=es[st][:, cols], in_=eg[st][:, t0 * 8 * P : t1 * 8 * P]
            )

        tb = const.tile([P, F], F32, name="tb")
        src_sb = const.tile([P, F], F32, name="src_sb")
        smean = const.tile([P, F], F32, name="smean")

        def x_product(s0, fh):
            cols = slice(H * fh, H * (fh + 1))
            pr = ps_acc.tile([P, H], F32, name="pr", tag="acc")
            for g in range(2):
                nc.tensor.matmul_mx(
                    out=pr[:],
                    lhsT=xc[:, g * P : (g + 1) * P].bitcast(X4),
                    lhsT_scale=xs[:, g * P : (g + 1) * P],
                    rhs=wc[s0 + g][:, cols].bitcast(X4),
                    rhs_scale=ws[s0 + g][:, cols],
                    start=(g == 0),
                    stop=(g == 1),
                )
            return pr

        def target_term(fh):
            cols = slice(H * fh, H * (fh + 1))
            pr = x_product(0, fh)
            nc.vector.tensor_tensor(out=tb[:, cols], in0=pr[:], in1=bias_bc[:, cols], op=ALU.add)

        def source_mean(fh):
            cols = slice(H * fh, H * (fh + 1))
            pr = x_product(2, fh)
            nc.scalar.copy(out=src_sb[:, cols], in_=pr[:])
            sm = ps_acc.tile([P, H], F32, name="sm", tag="acc")
            nc.tensor.matmul(out=sm[:], lhsT=blk[:], rhs=src_sb[:, cols], start=True, stop=True)
            nc.scalar.activation(out=smean[:, cols], in_=sm[:], func=ACT.Copy, scale=1.0 / N)

        vmax = {}
        vmin = {}
        qsum = {}
        zsum = {}
        for fh in range(2):
            vmax[fh] = const.tile([P, H], F32, name="vmax%d" % fh)
            vmin[fh] = const.tile([P, H], F32, name="vmin%d" % fh)
            qsum[fh] = const.tile([P, 2, H], F32, name="qsum%d" % fh)
            zsum[fh] = ps_sum.tile([P, H], F32, name="zsum%d" % fh)

        sqs = {}

        def e_passes(dst, j, fh, first, last):
            st, tl = j // JT, j % JT
            cols = slice(H * fh, H * (fh + 1))
            for g in range(2):
                one = slice((2 * tl + g) * P, (2 * tl + g + 1) * P)
                nc.tensor.matmul_mx(
                    out=dst[:],
                    lhsT=ec[st][:, one].bitcast(X4),
                    lhsT_scale=es[st][:, one],
                    rhs=wc[4 + g][:, cols].bitcast(X4),
                    rhs_scale=ws[4 + g][:, cols],
                    start=(first and g == 0),
                    stop=(last and g == 1),
                )

        def sum_passes(j, fh):
            e_passes(zsum[fh], j, fh, j == 0, j == N - 1)

        def open_bank(j, fh):
            acc = ps_acc.tile([P, H], F32, name="acc", tag="acc")
            e_passes(acc, j, fh, True, False)
            return acc

        def close_bank(acc, j, fh):
            st, tl = j // JT, j % JT
            cols = slice(H * fh, H * (fh + 1))
            for g in range(2):
                one = slice((2 * tl + g) * P, (2 * tl + g + 1) * P)
                nc.tensor.matmul_mx(
                    out=acc[:],
                    lhsT=xrc[st][:, one].bitcast(X4),
                    lhsT_scale=xrs[st][:, one],
                    rhs=wc[2 + g][:, cols].bitcast(X4),
                    rhs_scale=ws[2 + g][:, cols],
                    start=False,
                    stop=(g == 1),
                )
            if j == 0:
                nc.scalar.copy(out=vmax[fh][:], in_=acc[:])
                nc.scalar.activation(out=qsum[fh][:, 0, :], in_=acc[:], func=ACT.Square)
                return
            if j == 1:
                nc.vector.tensor_tensor(out=vmin[fh][:], in0=acc[:], in1=vmax[fh][:], op=ALU.min)
            else:
                nc.vector.tensor_tensor(out=vmin[fh][:], in0=acc[:], in1=vmin[fh][:], op=ALU.min)
            nc.vector.tensor_tensor(out=vmax[fh][:], in0=acc[:], in1=vmax[fh][:], op=ALU.max)
            if j == 1:
                nc.scalar.activation(out=qsum[fh][:, 1, :], in_=acc[:], func=ACT.Square)
                return
            if j % 2 == 0:
                sqs[fh] = sqpool.tile([P, 2, H], F32, name="sq", tag="sq")
            nc.scalar.activation(out=sqs[fh][:, j % 2, :], in_=acc[:], func=ACT.Square)
            if j % 2 == 1:
                nc.gpsimd.tensor_tensor(out=qsum[fh][:], in0=qsum[fh][:], in1=sqs[fh][:], op=ALU.add)

        def finish_minmax(fh):
            cols = slice(H * fh, H * (fh + 1))
            for a, v in ((1, vmin[fh]), (2, vmax[fh])):
                res = const.tile([P, H], F32, name="res%d_%d" % (a, fh))
                nc.vector.tensor_tensor(out=res[:], in0=v[:], in1=tb[:, cols], op=ALU.add)
                nc.sync.dma_start(out=out_view[:, a, cols], in_=res[:])

        def finish_sums(fh):
            cols = slice(H * fh, H * (fh + 1))
            mean = const.tile([P, H], F32, name="mean%d" % fh)
            std = const.tile([P, H], F32, name="std%d" % fh)
            mz = const.tile([P, H], F32, name="mz%d" % fh)
            msq = const.tile([P, H], F32, name="msq%d" % fh)
            var = const.tile([P, H], F32, name="var%d" % fh)
            nc.vector.scalar_tensor_tensor(
                out=mz[:], in0=zsum[fh][:], scalar=1.0 / N, in1=smean[:, cols], op0=ALU.mult, op1=ALU.add
            )
            nc.scalar.activation(out=msq[:], in_=mz[:], func=ACT.Square)
            nc.gpsimd.tensor_tensor(out=mean[:], in0=mz[:], in1=tb[:, cols], op=ALU.add)
            nc.sync.dma_start(out=out_view[:, 0, cols], in_=mean[:])
            nc.vector.scalar_tensor_tensor(
                out=var[:], in0=qsum[fh][:, 0, :], scalar=1.0 / N, in1=msq[:], op0=ALU.mult, op1=ALU.subtract
            )
            nc.vector.scalar_tensor_tensor(
                out=var[:], in0=qsum[fh][:, 1, :], scalar=1.0 / N, in1=var[:], op0=ALU.mult, op1=ALU.add
            )
            nc.vector.tensor_scalar(out=var[:], in0=var[:], scalar1=0.0, scalar2=EPS_STD, op0=ALU.max, op1=ALU.add)
            nc.scalar.activation(out=std[:], in_=var[:], func=ACT.Sqrt)
            nc.sync.dma_start(out=out_view[:, 3, cols], in_=std[:])

        def ahead(st, slot):
            if slot == 0 and st + 3 < NSTEP:
                load_e(st + 3)
            if st + 1 < NSTEP:
                if slot < JT:
                    widen(st + 1, slot)
                if slot == 1:
                    rep_x(st + 1)
                if slot == 2:
                    turn(st + 1, 1)
                    turn(st + 1, 2)
                if slot == 4:
                    turn(st + 1, 3)
                    turn(st + 1, 0)
                if slot == 6:
                    quant_e(st + 1, 0, JT)
            if st == 1 and slot == 0:
                nc.scalar.dma_start(out=bias_bc[:], in_=b_pre.partition_broadcast(P))
            if st == 0 and slot in (3, 7):
                source_mean((slot - 3) // 4)
            if st == 3 and slot == 0:
                for s, f2 in W_LATE:
                    load_w(s, f2)
            if st in (4, 5) and slot in (0, 1):
                s, f2 = W_LATE[2 * (st - 4) + slot]
                prep_w(s, f2, 0, 0, late=True)
            if st in (4, 5) and slot in (2, 4):
                s, f2 = W_LATE[2 * (st - 4) + (slot - 2) // 2]
                quant_w(s, f2)
            if st == 6 and slot in (5, 7):
                target_term((slot - 5) // 2)

        widen(0, 0)
        widen(0, 1)
        rep_x(0)
        turn(0, 0)
        turn(0, 1)
        prep_w(4, 0, CV, 0)
        prep_w(5, 0, CV, 0)
        quant_e(0, 0, 2)
        widen(0, 2)
        widen(0, 3)
        turn(0, 2)
        turn(0, 3)
        prep_w(2, 0, CV, 0)
        quant_e(0, 2, 4)
        prep_w(3, 0, CV, 0)
        first = {}
        for tl in range(JT):
            sum_passes(tl, 0)
            first[tl] = open_bank(tl, 0)
        for s, fh in W_URGENT[4:8]:
            prep_w(s, fh, 0, 0)
        for st in range(NSTEP):
            for fh in range(2):
                for tl in range(JT):
                    j = JT * st + tl
                    ahead(st, JT * fh + tl)
                    if st == 0 and fh == 0:
                        close_bank(first[tl], j, fh)
                        continue
                    if st < NSTEP - 1:
                        sum_passes(j, fh)
                    close_bank(open_bank(j, fh), j, fh)
                if st == NSTEP - 1:
                    finish_minmax(fh)
        for fh in range(2):
            for tl in range(JT):
                sum_passes(JT * (NSTEP - 1) + tl, fh)
            finish_sums(fh)
